import numpy as np
import ml_dtypes


def mxq(x, axis, fmt="e4m3"):
    dtype, down = {"e4m3": (ml_dtypes.float8_e4m3fn, 7), "e5m2": (ml_dtypes.float8_e5m2, 14)}[fmt]
    v = np.moveaxis(np.asarray(x, np.float32).astype(ml_dtypes.bfloat16).astype(np.float64), axis, -1)
    blocks = v.reshape(v.shape[:-1] + (-1, 32))
    amax = np.abs(blocks).max(-1, keepdims=True)
    byte = np.maximum(np.where(amax > 0, np.frexp(amax)[1] - 1 + 127, 0) - down, 1)
    scale = np.exp2(byte - 127.0)
    codes = (blocks / scale).astype(np.float32).astype(dtype).astype(np.float64)
    return np.moveaxis((codes * scale).reshape(v.shape), -1, axis)


WIDE = False


def mx_kscale(k):
    if not WIDE:
        return np.ones(k)
    levels = np.array([10, -10, 5, -5, 0])
    if k % 512:
        return np.exp2(np.random.permutation(np.resize(levels, k // 32))).repeat(32)
    a = np.empty((k // 512, 16))
    for p in range(k // 512):
        a[p, :8] = np.random.permutation(np.resize(levels, 8))
        for g in range(8):
            far = levels[np.abs(levels - a[p, g]) >= 10]
            a[p, g + 8] = far[np.random.randint(len(far))]
    return np.exp2(a.ravel()).repeat(32)


BF16 = ml_dtypes.bfloat16


def bf(x):
    return np.asarray(x, np.float32).astype(BF16)


def f64(x):
    return np.asarray(x).astype(np.float64)


B, S, D, BD, K = 4, 1024, 1024, 512, 128
TS = 3.0


def sigmoid(v):
    return 1.0 / (1.0 + np.exp(-v))


def draw0():
    s = mx_kscale(D)
    return {
        "token_embeddings": bf(np.random.standard_normal((B, S, D)) * TS * s),
        "splat_influences": bf(np.random.uniform(size=(B, S, K))),
        "decoded": bf(np.random.standard_normal((B, K, D)) * 0.35),
        "gate_W": bf(np.random.standard_normal((D, D)) / (TS * np.sqrt(D)) / s[:, None]),
        "gate_b": bf(np.random.standard_normal(D) * 0.5),
    }


def core(token_embeddings, splat_influences, decoded, gate_W, gate_b):
    flow = f64(splat_influences) @ f64(decoded)
    gate = sigmoid((mxq(f64(token_embeddings), 2, "e4m3") @ mxq(f64(gate_W), 0, "e4m3")) + f64(gate_b))
    return flow * gate


def e4m3fn_bytes(y):
    return np.clip(np.asarray(y, np.float64), -448.0, 448.0).astype(np.float32).astype(ml_dtypes.float8_e4m3fn).view(np.uint8)


def e4m3fn_values(b):
    return np.asarray(b, np.uint8).view(ml_dtypes.float8_e4m3fn).astype(np.float64)


def setup_inputs():
    d = draw0()
    x0 = np.asarray(d['token_embeddings']).astype(np.float64)
    s = (np.max(np.abs(x0), axis=(0, 1), keepdims=True) / 448.0).astype(np.float32)
    out = {}
    for k, v in d.items():
        if k == 'token_embeddings':
            out['token_embeddings_bytes'] = e4m3fn_bytes(x0 / s.astype(np.float64))
            out['token_embeddings_scale'] = s
        else:
            out[k] = v
    return out


def reference(token_embeddings_bytes, token_embeddings_scale, splat_influences, decoded, gate_W, gate_b):
    return core(e4m3fn_values(token_embeddings_bytes) * token_embeddings_scale.astype(np.float64), splat_influences, decoded, gate_W, gate_b)

@@ -1,0 +1,284 @@
+from contextlib import ExitStack
+
+import concourse.mybir as mybir
+from concourse.masks import make_identity
+
+B, S, D, KS = 4, 1024, 1024, 128
+FLOPS = 2 * B * S * D * D + 2 * B * S * KS * D
+
+F32 = mybir.dt.float32
+BF16 = mybir.dt.bfloat16
+U32 = mybir.dt.uint32
+U8 = mybir.dt.uint8
+FP8 = mybir.dt.float8_e4m3fn
+FP8X4 = mybir.dt.float8_e4m3fn_x4
+ACT = mybir.ActivationFunctionType
+ALU = mybir.AluOpType
+
+P = 128
+NG = 8
+NU = 32
+NQ = 32
+
+
+def tile_splatinformationflow_pb_kernel(tc, x_bytes, x_scale, infl, dec, gate_w, gate_b, out):
+    nc = tc.nc
+
+    x_view = x_bytes.rearrange("b (p h j) k -> b h p j k", h=2, j=4)
+    out_view = out.rearrange("b (p h j) n -> b h p j n", h=2, j=4)
+    infl_view = infl.rearrange("b (p q) k -> b p q k", q=8)
+    w_view = gate_w.rearrange("(g p t) n -> g p t n", g=2, t=4)
+
+    with ExitStack() as ctx:
+        keep = ctx.enter_context(tc.tile_pool(name="keep", bufs=1))
+        work = ctx.enter_context(tc.tile_pool(name="work", bufs=2))
+        psum = ctx.enter_context(tc.psum_pool(name="psum", bufs=2))
+        ctx.enter_context(tc.manual_schedule())
+
+        xb = []
+        for T in range(NG):
+            xb_t = keep.tile([P, 4, 1024], U8, name="xb%d" % T)
+            xb.append(xb_t)
+        sc = keep.tile([P, 1024], F32, name="sc")
+        wr = keep.tile([P, 2, 4, 1024], BF16, name="wr")
+        wg = keep.tile([P, 4, 2, 1024], BF16, name="wg", align_bytes=64)
+        wc = keep.tile([P, 4, 2, 256], U32, name="wc", align_bytes=64)
+        ws = keep.tile([P, 4, 2, 256], U8, name="ws", align_bytes=64)
+        inf = keep.tile([P, 4, 8, 128], BF16, name="inf")
+        inflT = keep.tile([P, 4096], BF16, name="inflT")
+        dc = keep.tile([P, 4, 1024], BF16, name="dc")
+        bias_bf = keep.tile([P, 8], BF16, name="bias_bf")
+        bias = keep.tile([P, 8], F32, name="bias")
+        ident_f = keep.tile([P, P], F32, name="ident_f")
+        ident_b = keep.tile([P, P], BF16, name="ident_b")
+        warm = keep.tile([P, 2], F32, name="warm")
+
+        nc.scalar.dma_start(out=sc[:], in_=x_scale.rearrange("a b k -> (a b k)").partition_broadcast(P))
+        with nc.allow_non_contiguous_dma(reason="1024 bias values, one to a partition and chunk"):
+            nc.scalar.dma_start(out=bias_bf[:], in_=gate_b.rearrange("(c p) -> p c", p=P))
+
+        def load_x(T):
+            nc.sync.dma_start(out=xb[T][:], in_=x_view[T // 2, T % 2])
+
+        def load_w(g, h):
+            nc.sync.dma_start(out=wr[:, g, :, 512 * h:512 * (h + 1)], in_=w_view[g][:, :, 512 * h:512 * (h + 1)])
+
+        def load_flow(b):
+            nc.sync.dma_start(out=inf[:, b], in_=infl_view[b])
+            nc.sync.dma_start(out=dc[:, b, :], in_=dec[b])
+
+        load_x(0)
+        load_w(0, 0)
+        load_w(1, 0)
+        load_flow(0)
+        load_x(1)
+        load_w(0, 1)
+        load_w(1, 1)
+        load_x(2)
+        load_flow(1)
+        load_x(3)
+        load_x(4)
+        load_flow(2)
+        load_x(5)
+        load_x(6)
+        load_flow(3)
+        load_x(7)
+
+        make_identity(nc, ident_f[:])
+        make_identity(nc, ident_b[:])
+        nc.vector.memset(warm[:], 0.0)
+        nc.scalar.activation(out=warm[:, 1:2], in_=warm[:, 0:1], func=ACT.Sigmoid)
+
+        xw = {}
+        gr = {}
+        xc = {}
+        xs = {}
+        xt = {}
+        acc = {}
+        fl = {}
+        gt = {}
+        ot_sb = {}
+        ot_ps = {}
+        o_sb = {}
+
+        def w_copy(eng, i):
+            dst = wg[:, i].rearrange("p g (n t) -> p g n t", t=4)
+            src = wr[:, :, :, 256 * i:256 * (i + 1)].rearrange("p g t n -> p g n t")
+            if eng == "S":
+                nc.scalar.copy(out=dst, in_=src)
+            else:
+                nc.vector.tensor_copy(out=dst, in_=src)
+
+        def w_quant(i):
+            nc.vector.quantize_mx(
+                out=wc[:, i].rearrange("p g n -> p (g n)").bitcast(FP8X4),
+                scales=ws[:, i].rearrange("p g n -> p (g n)"),
+                in_=wg[:, i].rearrange("p g c -> p (g c)"),
+            )
+
+        def widen(m):
+            T, j = m // 4, m % 4
+            if j == 0:
+                xw_t = work.tile([P, 4, 1024], BF16, name="xw", tag="xw", bufs=2)
+                xw[T] = xw_t
+            nc.vector.tensor_tensor(out=xw[T][:, j, :], in0=xb[T][:, j, :].bitcast(FP8), in1=sc[:], op=ALU.mult)
+
+        def x_transpose(m):
+            T, j = m // 4, m % 4
+            xt_t = psum.tile([P, 2, 2, 128], F32, name="xt", tag="xt", bufs=2)
+            xt[m] = xt_t
+            words = xw[T][:].rearrange("p j k -> p (j k)").bitcast(F32)
+            for g in range(2):
+                for u in range(2):
+                    lo = 512 * j + 256 * g
+                    nc.tensor.transpose(xt_t[:, g, u, :], words[:, lo + u:lo + 256:2], ident_f[:])
+
+        def x_evac(eng, m):
+            T, j = m // 4, m % 4
+            if j == 0:
+                gr_t = work.tile([P, 2, 2048], BF16, name="gr", tag="gr", bufs=2, align_bytes=64)
+                gr[T] = gr_t
+            gw = gr[T][:].rearrange("p g c -> p (g c)").bitcast(F32).rearrange("p (g r u) -> p g r u", g=2, u=2)
+            dst = gw[:, :, 128 * j:128 * (j + 1), :]
+            src = xt[m][:].rearrange("p g u r -> p g r u")
+            if eng == "S":
+                nc.scalar.copy(out=dst, in_=src)
+            else:
+                nc.vector.tensor_copy(out=dst, in_=src)
+
+        def x_quant(T):
+            xc_t = work.tile([P, 2, 512], U32, name="xc", tag="xc", bufs=2, align_bytes=64)
+            xs_t = work.tile([P, 2, 512], U8, name="xs", tag="xs", bufs=2, align_bytes=64)
+            xc[T] = xc_t
+            xs[T] = xs_t
+            nc.vector.quantize_mx(
+                out=xc_t[:].rearrange("p g n -> p (g n)").bitcast(FP8X4),
+                scales=xs_t[:].rearrange("p g n -> p (g n)"),
+                in_=gr[T][:].rearrange("p g c -> p (g c)"),
+            )
+
+        def infl_transpose(b):
+            it = psum.tile([P, 8, 128], BF16, name="it", tag="xt", bufs=2)
+            for j in range(8):
+                nc.tensor.transpose(it[:, j, :], inf[:, b, j, :], ident_b[:])
+            nc.scalar.copy(out=inflT[:, 1024 * b:1024 * (b + 1)], in_=it[:].rearrange("p j r -> p (j r)"))
+
+        def gate_mm(T, c):
+            acc_t = psum.tile([P, 512], F32, name="acc", tag="acc", bufs=2)
+            acc[c] = acc_t
+            for g in range(2):
+                nc.tensor.matmul_mx(
+                    out=acc_t[:],
+                    lhsT=wc[:, c // 2, g, 128 * (c % 2):128 * (c % 2 + 1)].bitcast(FP8X4),
+                    lhsT_scale=ws[:, c // 2, g, 128 * (c % 2):128 * (c % 2 + 1)],
+                    rhs=xc[T][:, g, :].bitcast(FP8X4),
+                    rhs_scale=xs[T][:, g, :],
+                    start=(g == 0),
+                    stop=(g == 1),
+                )
+
+        def sigmoid(c):
+            gt_t = work.tile([P, 512], F32, name="gt", tag="gt", bufs=3)
+            gt[c] = gt_t
+            nc.scalar.activation(out=gt_t[:], in_=acc[c][:], func=ACT.Sigmoid, bias=bias[:, c:c + 1], scale=1.0)
+
+        def flow_mm(T, c):
+            fl_t = psum.tile([P, 512], F32, name="fl", tag="fl", bufs=2)
+            fl[c] = fl_t
+            nc.tensor.matmul(
+                fl_t[:], lhsT=dc[:, T // 2, 128 * c:128 * (c + 1)], rhs=inflT[:, 512 * T:512 * (T + 1)],
+                start=True, stop=True,
+            )
+
+        def product(T, c):
+            ot_t = work.tile([P, 512], F32, name="ot_sb", tag="ot_sb", bufs=4)
+            ot_sb[(T, c)] = ot_t
+            nc.vector.tensor_tensor(out=ot_t[:], in0=fl[c][:], in1=gt[c][:], op=ALU.mult)
+
+        def o_transpose(T, c):
+            ps = psum.tile([P, 4, 128], F32, name="ot_ps", tag="ot_ps", bufs=2)
+            ot_ps[(T, c)] = ps
+            for j in range(4):
+                nc.tensor.transpose(ps[:, j, :], ot_sb[(T, c)][:, 128 * j:128 * (j + 1)], ident_f[:])
+
+        def o_evac(eng, T, c):
+            if c == 0:
+                o_t = work.tile([P, 4, 1024], F32, name="o_sb", tag="o_sb", bufs=3)
+                o_sb[T] = o_t
+            if eng == "S":
+                nc.scalar.copy(out=o_sb[T][:, :, 128 * c:128 * (c + 1)], in_=ot_ps[(T, c)][:])
+            else:
+                nc.vector.tensor_copy(out=o_sb[T][:, :, 128 * c:128 * (c + 1)], in_=ot_ps[(T, c)][:])
+
+        def store(T, c_lo, c_hi):
+            nc.sync.dma_start(
+                out=out_view[T // 2, T % 2][:, :, 128 * c_lo:128 * c_hi],
+                in_=o_sb[T][:, :, 128 * c_lo:128 * c_hi],
+            )
+
+        DX = 5
+        W_ENGINE = "SVS"
+        w_copy("S", 0)
+        for m in range(4):
+            widen(m)
+        x_transpose(0)
+        x_transpose(1)
+        x_evac("S", 0)
+        x_transpose(2)
+        x_evac("S", 1)
+        x_transpose(3)
+        x_evac("S", 2)
+        w_quant(0)
+        nc.vector.tensor_copy(out=bias[:], in_=bias_bf[:])
+        x_evac("S", 3)
+        infl_transpose(0)
+        x_quant(0)
+        widen(4)
+        n_wide, n_tr, n_ev, n_quant = 5, 4, 4, 1
+
+        for q in range(0, NQ + 1):
+            T, pi = q // 4, q % 4
+            c0, c1 = 2 * pi, 2 * pi + 1
+            live = q < NQ
+            while n_ev < n_tr:
+                x_evac("V" if (q >= 4 and pi in (1, 2)) else "S", n_ev)
+                n_ev += 1
+            if q < 3:
+                w_copy(W_ENGINE[q], q + 1)
+                w_quant(q + 1)
+            if live:
+                gate_mm(T, c0)
+                gate_mm(T, c1)
+                sigmoid(c0)
+                sigmoid(c1)
+                flow_mm(T, c0)
+                flow_mm(T, c1)
+            if n_quant < NG and n_ev >= 4 * n_quant + 4:
+                x_quant(n_quant)
+                n_quant += 1
+            if live:
+                product(T, c0)
+                product(T, c1)
+            if q >= 1:
+                Tp, pp = (q - 1) // 4, (q - 1) % 4
+                o_transpose(Tp, 2 * pp)
+                o_transpose(Tp, 2 * pp + 1)
+            started = 0
+            while n_tr < min(NU, q + DX + 1, n_wide) and started < 2:
+                x_transpose(n_tr)
+                n_tr += 1
+                started += 1
+            if q >= 1:
+                o_evac("S", Tp, 2 * pp)
+                o_evac("V" if q == NQ else "S", Tp, 2 * pp + 1)
+                if Tp == NG - 1:
+                    store(Tp, 2 * pp, 2 * pp + 2)
+                elif pp % 2 == 1:
+                    store(Tp, 2 * pp - 2, 2 * pp + 2)
+            if q % 8 == 4 and q // 8 + 1 < B:
+                infl_transpose(q // 8 + 1)
+            started = 0
+            while n_wide < min(NU, q + DX + 2) and started < 2:
+                widen(n_wide)
+                n_wide += 1
+                started += 1

@@ -60,20 +60,26 @@ def tile_splatinformationflow_pb_kernel(tc, x_bytes, x_scale, infl, dec, gate_w,
         def load_x(T):
             nc.sync.dma_start(out=xb[T][:], in_=x_view[T // 2, T % 2])
 
-        def load_w(g, h):
-            nc.sync.dma_start(out=wr[:, g, :, 512 * h:512 * (h + 1)], in_=w_view[g][:, :, 512 * h:512 * (h + 1)])
+        def load_x_unit(T, j):
+            nc.sync.dma_start(out=xb[T][:, j, :], in_=x_view[T // 2, T % 2][:, j, :])
+
+        def load_w(g, lo, hi):
+            nc.sync.dma_start(out=wr[:, g, :, lo:hi], in_=w_view[g][:, :, lo:hi])
 
         def load_flow(b):
             nc.sync.dma_start(out=inf[:, b], in_=infl_view[b])
             nc.sync.dma_start(out=dc[:, b, :], in_=dec[b])
 
-        load_x(0)
-        load_w(0, 0)
-        load_w(1, 0)
+        for j in range(4):
+            load_x_unit(0, j)
+        load_w(0, 0, 256)
+        load_w(1, 0, 256)
         load_flow(0)
+        load_w(0, 256, 512)
+        load_w(1, 256, 512)
         load_x(1)
-        load_w(0, 1)
-        load_w(1, 1)
+        load_w(0, 512, 1024)
+        load_w(1, 512, 1024)
         load_x(2)
         load_flow(1)
         load_x(3)
@@ -101,9 +107,9 @@ def tile_splatinformationflow_pb_kernel(tc, x_bytes, x_scale, infl, dec, gate_w,
         ot_ps = {}
         o_sb = {}
 
-        def w_copy(eng, i):
-            dst = wg[:, i].rearrange("p g (n t) -> p g n t", t=4)
-            src = wr[:, :, :, 256 * i:256 * (i + 1)].rearrange("p g t n -> p g n t")
+        def w_copy(eng, i, g):
+            dst = wg[:, i, g].rearrange("p (n t) -> p n t", t=4)
+            src = wr[:, g, :, 256 * i:256 * (i + 1)].rearrange("p t n -> p n t")
             if eng == "S":
                 nc.scalar.copy(out=dst, in_=src)
             else:
@@ -156,6 +162,19 @@ def tile_splatinformationflow_pb_kernel(tc, x_bytes, x_scale, infl, dec, gate_w,
                 scales=xs_t[:].rearrange("p g n -> p (g n)"),
                 in_=gr[T][:].rearrange("p g c -> p (g c)"),
             )
+
+        def x_quant_half(T, half):
+            if half == 0:
+                xc_t = work.tile([P, 2, 512], U32, name="xc", tag="xc", bufs=2, align_bytes=64)
+                xs_t = work.tile([P, 2, 512], U8, name="xs", tag="xs", bufs=2, align_bytes=64)
+                xc[T] = xc_t
+                xs[T] = xs_t
+            for g in range(2):
+                nc.vector.quantize_mx(
+                    out=xc[T][:, g, 256 * half:256 * (half + 1)].bitcast(FP8X4),
+                    scales=xs[T][:, g, 256 * half:256 * (half + 1)],
+                    in_=gr[T][:, g, 1024 * half:1024 * (half + 1)],
+                )
 
         def infl_transpose(b):
             it = psum.tile([P, 8, 128], BF16, name="it", tag="xt", bufs=2)
@@ -217,22 +236,23 @@ def tile_splatinformationflow_pb_kernel(tc, x_bytes, x_scale, infl, dec, gate_w,
             )
 
         DX = 5
-        W_ENGINE = "SVS"
-        w_copy("S", 0)
         for m in range(4):
             widen(m)
         x_transpose(0)
         x_transpose(1)
         x_evac("S", 0)
-        x_transpose(2)
+        w_copy("S", 0, 0)
         x_evac("S", 1)
-        x_transpose(3)
+        x_transpose(2)
         x_evac("S", 2)
+        x_transpose(3)
+        w_copy("V", 0, 1)
+        x_quant_half(0, 0)
         w_quant(0)
         nc.vector.tensor_copy(out=bias[:], in_=bias_bf[:])
         x_evac("S", 3)
         infl_transpose(0)
-        x_quant(0)
+        x_quant_half(0, 1)
         widen(4)
         n_wide, n_tr, n_ev, n_quant = 5, 4, 4, 1
 
@@ -244,8 +264,8 @@ def tile_splatinformationflow_pb_kernel(tc, x_bytes, x_scale, infl, dec, gate_w,
                 x_evac("V" if (q >= 4 and pi in (1, 2)) else "S", n_ev)
                 n_ev += 1
             if q < 3:
-                w_copy(W_ENGINE[q], q + 1)
-                w_quant(q + 1)
+                w_copy("S", q + 1, 0)
+                w_copy("V", q + 1, 1)
             if live:
                 gate_mm(T, c0)
                 gate_mm(T, c1)
@@ -253,6 +273,8 @@ def tile_splatinformationflow_pb_kernel(tc, x_bytes, x_scale, infl, dec, gate_w,
                 sigmoid(c1)
                 flow_mm(T, c0)
                 flow_mm(T, c1)
+            if q < 3:
+                w_quant(q + 1)
             if n_quant < NG and n_ev >= 4 * n_quant + 4:
                 x_quant(n_quant)
                 n_quant += 1
@@ -269,7 +291,7 @@ def tile_splatinformationflow_pb_kernel(tc, x_bytes, x_scale, infl, dec, gate_w,
                 n_tr += 1
                 started += 1
             if q >= 1:
-                o_evac("S", Tp, 2 * pp)
+                o_evac("V" if False else "S", Tp, 2 * pp)
                 o_evac("V" if q == NQ else "S", Tp, 2 * pp + 1)
                 if Tp == NG - 1:
                     store(Tp, 2 * pp, 2 * pp + 2)

@@ -214,8 +214,8 @@ def tile_splatinformationflow_pb_kernel(tc, x_bytes, x_scale, infl, dec, gate_w,
             ot_sb[(T, c)] = ot_t
             nc.vector.tensor_tensor(out=ot_t[:], in0=fl[c][:], in1=gt[c][:], op=ALU.mult)
 
-        def o_transpose(T, c):
-            ps = psum.tile([P, 4, 128], F32, name="ot_ps", tag="ot_ps", bufs=2)
+        def o_transpose(T, c, tag="ot_ps"):
+            ps = psum.tile([P, 4, 128], F32, name="ot_ps", tag=tag, bufs=2)
             ot_ps[(T, c)] = ps
             for j in range(4):
                 nc.tensor.transpose(ps[:, j, :], ot_sb[(T, c)][:, 128 * j:128 * (j + 1)], ident_f[:])
@@ -283,8 +283,8 @@ def tile_splatinformationflow_pb_kernel(tc, x_bytes, x_scale, infl, dec, gate_w,
                 product(T, c1)
             if q >= 1:
                 Tp, pp = (q - 1) // 4, (q - 1) % 4
-                o_transpose(Tp, 2 * pp)
-                o_transpose(Tp, 2 * pp + 1)
+                o_transpose(Tp, 2 * pp, "xt" if q == NQ else "ot_ps")
+                o_transpose(Tp, 2 * pp + 1, "xt" if q == NQ else "ot_ps")
             started = 0
             while n_tr < min(NU, q + DX + 1, n_wide) and started < 2:
                 x_transpose(n_tr)
@@ -292,8 +292,12 @@ def tile_splatinformationflow_pb_kernel(tc, x_bytes, x_scale, infl, dec, gate_w,
                 started += 1
             if q >= 1:
                 o_evac("V" if False else "S", Tp, 2 * pp)
-                o_evac("V" if q == NQ else "S", Tp, 2 * pp + 1)
-                if Tp == NG - 1:
+                if q == NQ:
+                    store(Tp, 2 * pp, 2 * pp + 1)
+                o_evac("V" if q >= 29 else "S", Tp, 2 * pp + 1)
+                if q == NQ:
+                    store(Tp, 2 * pp + 1, 2 * pp + 2)
+                elif Tp == NG - 1:
                     store(Tp, 2 * pp, 2 * pp + 2)
                 elif pp % 2 == 1:
                     store(Tp, 2 * pp - 2, 2 * pp + 2)

@@ -47,15 +47,15 @@ def tile_splatinformationflow_pb_kernel(tc, x_bytes, x_scale, infl, dec, gate_w,
         inf = keep.tile([P, 4, 8, 128], BF16, name="inf")
         inflT = keep.tile([P, 4096], BF16, name="inflT")
         dc = keep.tile([P, 4, 1024], BF16, name="dc")
-        bias_bf = keep.tile([P, 8], BF16, name="bias_bf")
+        brows = keep.tile([P, P], BF16, name="brows")
         bias = keep.tile([P, 8], F32, name="bias")
         ident_f = keep.tile([P, P], F32, name="ident_f")
         ident_b = keep.tile([P, P], BF16, name="ident_b")
         warm = keep.tile([P, 2], F32, name="warm")
 
         nc.scalar.dma_start(out=sc[:], in_=x_scale.rearrange("a b k -> (a b k)").partition_broadcast(P))
-        with nc.allow_non_contiguous_dma(reason="1024 bias values, one to a partition and chunk"):
-            nc.scalar.dma_start(out=bias_bf[:], in_=gate_b.rearrange("(c p) -> p c", p=P))
+        nc.gpsimd.memset(brows[:], 0.0)
+        nc.scalar.dma_start(out=brows[0:8, :], in_=gate_b.rearrange("(c n) -> c n", n=P))
 
         def load_x(T):
             nc.sync.dma_start(out=xb[T][:], in_=x_view[T // 2, T % 2])
@@ -236,6 +236,8 @@ def tile_splatinformationflow_pb_kernel(tc, x_bytes, x_scale, infl, dec, gate_w,
             )
 
         DX = 5
+        bt = psum.tile([P, P], BF16, name="bt", tag="acc", bufs=2)
+        nc.tensor.transpose(bt[:], brows[:], ident_b[:])
         for m in range(4):
             widen(m)
         x_transpose(0)
@@ -249,7 +251,7 @@ def tile_splatinformationflow_pb_kernel(tc, x_bytes, x_scale, infl, dec, gate_w,
         w_copy("V", 0, 1)
         x_quant_half(0, 0)
         w_quant(0)
-        nc.vector.tensor_copy(out=bias[:], in_=bias_bf[:])
+        nc.vector.tensor_copy(out=bias[:], in_=bt[:, 0:8])
         x_evac("S", 3)
         infl_transpose(0)
         x_quant_half(0, 1)

@@ -18,6 +18,7 @@ ALU = mybir.AluOpType
 P = 128
 NG = 8
 NU = 32
+FIRST_ORDERED = 8
 NQ = 32
 
 
@@ -96,6 +97,7 @@ def tile_splatinformationflow_pb_kernel(tc, x_bytes, x_scale, infl, dec, gate_w,
         nc.scalar.activation(out=warm[:, 1:2], in_=warm[:, 0:1], func=ACT.Sigmoid)
 
         xw = {}
+        xp = {}
         gr = {}
         xc = {}
         xs = {}
@@ -129,6 +131,17 @@ def tile_splatinformationflow_pb_kernel(tc, x_bytes, x_scale, infl, dec, gate_w,
                 xw[T] = xw_t
             nc.vector.tensor_tensor(out=xw[T][:, j, :], in0=xb[T][:, j, :].bitcast(FP8), in1=sc[:], op=ALU.mult)
 
+        def x_order(m):
+            T, j = m // 4, m % 4
+            if j == 0:
+                xp_t = work.tile([P, 4, 2, 2, 128], F32, name="xp", tag="xp", bufs=2)
+                xp[T] = xp_t
+            words = xw[T][:].rearrange("p j k -> p (j k)").bitcast(F32)
+            nc.gpsimd.tensor_copy(
+                out=xp[T][:, j],
+                in_=words[:, 512 * j:512 * (j + 1)].rearrange("p (g i u) -> p g u i", g=2, u=2),
+            )
+
         def x_transpose(m):
             T, j = m // 4, m % 4
             xt_t = psum.tile([P, 2, 2, 128], F32, name="xt", tag="xt", bufs=2)
@@ -137,7 +150,8 @@ def tile_splatinformationflow_pb_kernel(tc, x_bytes, x_scale, infl, dec, gate_w,
             for g in range(2):
                 for u in range(2):
                     lo = 512 * j + 256 * g
-                    nc.tensor.transpose(xt_t[:, g, u, :], words[:, lo + u:lo + 256:2], ident_f[:])
+                    src = xp[T][:, j, g, u, :] if m >= FIRST_ORDERED else words[:, lo + u:lo + 256:2]
+                    nc.tensor.transpose(xt_t[:, g, u, :], src, ident_f[:])
 
         def x_evac(eng, m):
             T, j = m // 4, m % 4
@@ -306,7 +320,9 @@ def tile_splatinformationflow_pb_kernel(tc, x_bytes, x_scale, infl, dec, gate_w,
             if q % 8 == 4 and q // 8 + 1 < B:
                 infl_transpose(q // 8 + 1)
             started = 0
-            while n_wide < min(NU, q + DX + 2) and started < 2:
+            while n_wide < min(NU, q + DX + (3 if q >= 6 else 2)) and started < 2:
                 widen(n_wide)
+                if n_wide >= FIRST_ORDERED:
+                    x_order(n_wide)
                 n_wide += 1
                 started += 1

@@ -4,6 +4,23 @@ import concourse.mybir as mybir
 from concourse.masks import make_identity
 
 B, S, D, KS = 4, 1024, 1024, 128
+def SLOT(q):
+    if q < 0 or q >= 32:
+        return ()
+    T, pi = q // 4, q % 4
+    if T == 7:
+        return tuple((c, "R" if c in LASTR else "F") for c in LASTS[pi])
+    return tuple((c, "R" if (T >= R0 and c == 2 * RP + 1) else "F") for c in (2 * pi, 2 * pi + 1))
+
+
+def XLIM(q):
+    return XA[q] if q < len(XA) else max(XA[-1], q + 6 - XB)
+
+
+def WLIM(q):
+    return WA[q] if q < len(WA) else max(WA[-1], q + 6 - XB + WB)
+
+
 FLOPS = 2 * B * S * D * D + 2 * B * S * KS * D
 
 F32 = mybir.dt.float32
@@ -18,7 +35,35 @@ ALU = mybir.AluOpType
 P = 128
 NG = 8
 NU = 32
-FIRST_ORDERED = 8
+VE = (3,)
+XA = (6, 8, 9)
+WA = (7, 9, 10)
+XB = -1
+WB = 2
+ORD = 1
+SEQ = [(0, 0), (0, 1), (0, 2), (0, 3), (1, 0), (1, 1), (1, 2), (1, 3)] if ORD == 0 else [(0, 0), (0, 1), (0, 2), (1, 0), (1, 1), (1, 2), (0, 3), (1, 3)] if ORD == 1 else [(0, 0), (0, 1), (1, 0), (1, 1), (0, 2), (1, 2), (0, 3), (1, 3)]
+SEQ = SEQ + [(t, p) for t in range(2, 8) for p in range(4)]
+WAT = (0, 1, 2)
+EVN = ()
+EVE = "S"
+WC = ('V', 'V', 'V', 'S')
+ST = 2
+TB = 1
+LASTV = 0
+LASTS = ((0, 4), (1, 2), (3, 5), (6, 7))
+LASTR = (3, 4, 5, 6, 7)
+RP = 3
+R0 = 9
+HEAD = 1
+EV3 = 'S'
+W4 = 0
+WPOS = (0, 1)
+QV = 4
+QL = 99
+QE = 99
+IT = (3, 10, 18)
+QA = 0
+FIRST_ORDERED = 12
 NQ = 32
 
 
@@ -50,6 +95,7 @@ def tile_splatinformationflow_pb_kernel(tc, x_bytes, x_scale, infl, dec, gate_w,
         dc = keep.tile([P, 4, 1024], BF16, name="dc")
         brows = keep.tile([P, P], BF16, name="brows")
         bias = keep.tile([P, 8], F32, name="bias")
+        brow = keep.tile([P, 1024], BF16, name="brow")
         ident_f = keep.tile([P, P], F32, name="ident_f")
         ident_b = keep.tile([P, P], BF16, name="ident_b")
         warm = keep.tile([P, 2], F32, name="warm")
@@ -71,16 +117,23 @@ def tile_splatinformationflow_pb_kernel(tc, x_bytes, x_scale, infl, dec, gate_w,
             nc.sync.dma_start(out=inf[:, b], in_=infl_view[b])
             nc.sync.dma_start(out=dc[:, b, :], in_=dec[b])
 
-        for j in range(4):
-            load_x_unit(0, j)
-        load_w(0, 0, 256)
-        load_w(1, 0, 256)
+        if HEAD == 0:
+            for j in range(4):
+                load_x_unit(0, j)
+            load_w(0, 0, 256)
+            load_w(1, 0, 256)
+        else:
+            for j in range(4):
+                load_x_unit(0, j)
+                if j in WPOS:
+                    load_w(WPOS.index(j), 0, 256)
         load_flow(0)
         load_w(0, 256, 512)
         load_w(1, 256, 512)
         load_x(1)
         load_w(0, 512, 1024)
         load_w(1, 512, 1024)
+        nc.sync.dma_start(out=brow[:], in_=gate_b.partition_broadcast(P))
         load_x(2)
         load_flow(1)
         load_x(3)
@@ -167,8 +220,8 @@ def tile_splatinformationflow_pb_kernel(tc, x_bytes, x_scale, infl, dec, gate_w,
                 nc.vector.tensor_copy(out=dst, in_=src)
 
         def x_quant(T):
-            xc_t = work.tile([P, 2, 512], U32, name="xc", tag="xc", bufs=2, align_bytes=64)
-            xs_t = work.tile([P, 2, 512], U8, name="xs", tag="xs", bufs=2, align_bytes=64)
+            xc_t = work.tile([P, 2, 512], U32, name="xc", tag="xc", bufs=3, align_bytes=64)
+            xs_t = work.tile([P, 2, 512], U8, name="xs", tag="xs", bufs=3, align_bytes=64)
             xc[T] = xc_t
             xs[T] = xs_t
             nc.vector.quantize_mx(
@@ -179,8 +232,8 @@ def tile_splatinformationflow_pb_kernel(tc, x_bytes, x_scale, infl, dec, gate_w,
 
         def x_quant_half(T, half):
             if half == 0:
-                xc_t = work.tile([P, 2, 512], U32, name="xc", tag="xc", bufs=2, align_bytes=64)
-                xs_t = work.tile([P, 2, 512], U8, name="xs", tag="xs", bufs=2, align_bytes=64)
+                xc_t = work.tile([P, 2, 512], U32, name="xc", tag="xc", bufs=3, align_bytes=64)
+                xs_t = work.tile([P, 2, 512], U8, name="xs", tag="xs", bufs=3, align_bytes=64)
                 xc[T] = xc_t
                 xs[T] = xs_t
             for g in range(2):
@@ -235,13 +288,61 @@ def tile_splatinformationflow_pb_kernel(tc, x_bytes, x_scale, infl, dec, gate_w,
                 nc.tensor.transpose(ps[:, j, :], ot_sb[(T, c)][:, 128 * j:128 * (j + 1)], ident_f[:])
 
         def o_evac(eng, T, c):
-            if c == 0:
-                o_t = work.tile([P, 4, 1024], F32, name="o_sb", tag="o_sb", bufs=3)
-                o_sb[T] = o_t
+            o_tile(T)
             if eng == "S":
                 nc.scalar.copy(out=o_sb[T][:, :, 128 * c:128 * (c + 1)], in_=ot_ps[(T, c)][:])
             else:
                 nc.vector.tensor_copy(out=o_sb[T][:, :, 128 * c:128 * (c + 1)], in_=ot_ps[(T, c)][:])
+
+        def row_mm(T, c):
+            z_t = psum.tile([P, 4, 128], F32, name="acc", tag="acc", bufs=2)
+            acc[c] = z_t
+            lo = 128 * (c % 2)
+            for j in range(4):
+                for g in range(2):
+                    nc.tensor.matmul_mx(
+                        out=z_t[:, j, :],
+                        lhsT=xc[T][:, g, 128 * j:128 * (j + 1)].bitcast(FP8X4),
+                        lhsT_scale=xs[T][:, g, 128 * j:128 * (j + 1)],
+                        rhs=wc[:, c // 2, g, lo:lo + 128].bitcast(FP8X4),
+                        rhs_scale=ws[:, c // 2, g, lo:lo + 128],
+                        start=(g == 0),
+                        stop=(g == 1),
+                    )
+
+        def row_add(c):
+            zb_t = work.tile([P, 4, 128], F32, name="zb", tag="zb", bufs=2)
+            gt[c] = zb_t
+            nc.vector.tensor_tensor(
+                out=zb_t[:], in0=acc[c][:],
+                in1=brow[:, 128 * c:128 * (c + 1)].unsqueeze(1).to_broadcast([P, 4, 128]), op=ALU.add,
+            )
+
+        def row_sigmoid(c):
+            g_t = work.tile([P, 4, 128], F32, name="gt", tag="gt", bufs=3)
+            nc.scalar.activation(out=g_t[:], in_=gt[c][:], func=ACT.Sigmoid)
+            gt[c] = g_t
+
+        def row_flow(T, c):
+            fl_t = psum.tile([P, 4, 128], F32, name="fl", tag="fl", bufs=2)
+            fl[c] = fl_t
+            for j in range(4):
+                lo = 512 * T + 128 * j
+                nc.tensor.matmul(
+                    fl_t[:, j, :], lhsT=inflT[:, lo:lo + 128], rhs=dc[:, T // 2, 128 * c:128 * (c + 1)],
+                    start=True, stop=True,
+                )
+
+        def o_tile(T):
+            if T not in o_sb:
+                o_t = work.tile([P, 4, 1024], F32, name="o_sb", tag="o_sb", bufs=3)
+                o_sb[T] = o_t
+            return o_sb[T]
+
+        def row_product(T, c):
+            nc.vector.tensor_tensor(
+                out=o_tile(T)[:, :, 128 * c:128 * (c + 1)], in0=fl[c][:], in1=gt[c][:], op=ALU.mult,
+            )
 
         def store(T, c_lo, c_hi):
             nc.sync.dma_start(
@@ -249,80 +350,133 @@ def tile_splatinformationflow_pb_kernel(tc, x_bytes, x_scale, infl, dec, gate_w,
                 in_=o_sb[T][:, :, 128 * c_lo:128 * c_hi],
             )
 
-        DX = 5
         bt = psum.tile([P, P], BF16, name="bt", tag="acc", bufs=2)
         nc.tensor.transpose(bt[:], brows[:], ident_b[:])
-        for m in range(4):
-            widen(m)
-        x_transpose(0)
-        x_transpose(1)
-        x_evac("S", 0)
-        w_copy("S", 0, 0)
-        x_evac("S", 1)
-        x_transpose(2)
-        x_evac("S", 2)
-        x_transpose(3)
-        w_copy("V", 0, 1)
-        x_quant_half(0, 0)
-        w_quant(0)
-        nc.vector.tensor_copy(out=bias[:], in_=bt[:, 0:8])
-        x_evac("S", 3)
-        infl_transpose(0)
-        x_quant_half(0, 1)
-        widen(4)
+        if HEAD == 0:
+            for m in range(4):
+                widen(m)
+            x_transpose(0)
+            x_transpose(1)
+            x_evac("S", 0)
+            w_copy("S", 0, 0)
+            x_evac("S", 1)
+            x_transpose(2)
+            x_evac("S", 2)
+            x_transpose(3)
+            w_copy("V", 0, 1)
+            x_quant_half(0, 0)
+            w_quant(0)
+            nc.vector.tensor_copy(out=bias[:], in_=bt[:, 0:8])
+            x_evac("S", 3)
+            infl_transpose(0)
+            x_quant_half(0, 1)
+            widen(4)
+        else:
+            widen(0)
+            widen(1)
+            widen(2)
+            widen(3)
+            w_copy("S", 0, 0)
+            x_transpose(0)
+            if HEAD == 1:
+                w_copy("S", 0, 1)
+                x_evac("S", 0)
+            else:
+                x_evac("S", 0)
+                w_copy("S", 0, 1)
+            x_transpose(1)
+            x_evac("S", 1)
+            x_transpose(2)
+            x_evac("S", 2)
+            x_transpose(3)
+            w_quant(0)
+            x_quant_half(0, 0)
+            nc.vector.tensor_copy(out=bias[:], in_=bt[:, 0:8])
+            if EV3 == "V":
+                widen(4) if W4 else None
+            x_evac(EV3, 3)
+            infl_transpose(0)
+            x_quant_half(0, 1)
+            if not (EV3 == "V" and W4):
+                widen(4)
         n_wide, n_tr, n_ev, n_quant = 5, 4, 4, 1
 
         for q in range(0, NQ + 1):
-            T, pi = q // 4, q % 4
-            c0, c1 = 2 * pi, 2 * pi + 1
-            live = q < NQ
+            T = q // 4
+            slots = SLOT(q)
+            prev = SLOT(q - 1)
+            Tp = (q - 1) // 4
+            late = []
             while n_ev < n_tr:
-                x_evac("V" if (q >= 4 and pi in (1, 2)) else "S", n_ev)
+                if q >= QV and q % 4 in VE:
+                    x_evac("V", n_ev)
+                elif q >= QL:
+                    late.append(n_ev)
+                else:
+                    x_evac("S", n_ev)
                 n_ev += 1
-            if q < 3:
-                w_copy("S", q + 1, 0)
-                w_copy("V", q + 1, 1)
-            if live:
-                gate_mm(T, c0)
-                gate_mm(T, c1)
-                sigmoid(c0)
-                sigmoid(c1)
-                flow_mm(T, c0)
-                flow_mm(T, c1)
-            if q < 3:
-                w_quant(q + 1)
-            if n_quant < NG and n_ev >= 4 * n_quant + 4:
+            for i in range(1, 4):
+                if q == WAT[i - 1]:
+                    w_copy("S", i, 0)
+                    w_copy(WC[i], i, 1)
+            for c, form in slots:
+                (gate_mm if form == "F" else row_mm)(T, c)
+            for c, form in slots:
+                if form == "R":
+                    row_add(c)
+            for c, form in slots:
+                (sigmoid if form == "F" else row_sigmoid)(c)
+            for c, form in slots:
+                (flow_mm if form == "F" else row_flow)(T, c)
+            for e in late:
+                x_evac("S", e)
+            for i in range(1, 4):
+                if q == WAT[i - 1]:
+                    w_quant(i)
+            doq = n_quant < NG and n_ev >= 4 * n_quant + 4
+            if doq and q < QE:
                 x_quant(n_quant)
                 n_quant += 1
-            if live:
-                product(T, c0)
-                product(T, c1)
-            if q >= 1:
-                Tp, pp = (q - 1) // 4, (q - 1) % 4
-                o_transpose(Tp, 2 * pp, "xt" if q == NQ else "ot_ps")
-                o_transpose(Tp, 2 * pp + 1, "xt" if q == NQ else "ot_ps")
+                doq = False
+            for c, form in slots:
+                (product if form == "F" else row_product)(T, c)
+            if q >= 28:
+                for c, form in slots:
+                    if form == "R":
+                        store(T, c, c + 1)
+            for c, form in prev:
+                if form == "F":
+                    o_transpose(Tp, c, "xt" if q == NQ else "ot_ps")
             started = 0
-            while n_tr < min(NU, q + DX + 1, n_wide) and started < 2:
+            while n_tr < min(NU, XLIM(q), n_wide) and started < 2:
                 x_transpose(n_tr)
                 n_tr += 1
                 started += 1
-            if q >= 1:
-                o_evac("V" if False else "S", Tp, 2 * pp)
-                if q == NQ:
-                    store(Tp, 2 * pp, 2 * pp + 1)
-                o_evac("V" if q >= 29 else "S", Tp, 2 * pp + 1)
-                if q == NQ:
-                    store(Tp, 2 * pp + 1, 2 * pp + 2)
-                elif Tp == NG - 1:
-                    store(Tp, 2 * pp, 2 * pp + 2)
-                elif pp % 2 == 1:
-                    store(Tp, 2 * pp - 2, 2 * pp + 2)
-            if q % 8 == 4 and q // 8 + 1 < B:
-                infl_transpose(q // 8 + 1)
+            if q in EVN:
+                while n_ev < n_tr:
+                    x_evac(EVE, n_ev)
+                    n_ev += 1
+                doq = n_quant < NG and n_ev >= 4 * n_quant + 4
+            for s, (c, form) in enumerate(prev):
+                if form == "F":
+                    o_evac("V" if s == 1 and q >= 29 and LASTV else "S", Tp, c)
+                    if Tp == NG - 1:
+                        store(Tp, c, c + 1)
+            if q >= 1 and Tp < NG - 1 and (q - 1) % 2 == 1:
+                store(Tp, 4 * ((q - 1) % 4 // 2), 4 * ((q - 1) % 4 // 2) + 4)
+            if q in IT:
+                infl_transpose(IT.index(q) + 1)
+            if doq and QA == 0:
+                x_quant(n_quant)
+                n_quant += 1
+                doq = False
             started = 0
-            while n_wide < min(NU, q + DX + (3 if q >= 6 else 2)) and started < 2:
+            while n_wide < min(NU, WLIM(q)) and started < ST:
                 widen(n_wide)
                 if n_wide >= FIRST_ORDERED:
                     x_order(n_wide)
                 n_wide += 1
                 started += 1
+            if doq and QA == 1:
+                x_quant(n_quant)
+                n_quant += 1

@@ -10,7 +10,12 @@ def SLOT(q):
     T, pi = q // 4, q % 4
     if T == 7:
         return tuple((c, "R" if c in LASTR else "F") for c in LASTS[pi])
-    return tuple((c, "R" if (T >= R0 and c == 2 * RP + 1) else "F") for c in (2 * pi, 2 * pi + 1))
+    if T == 6 and PENR:
+        return tuple((c, "R" if c in PENR else "F") for c in PENS[pi])
+    pair = (2 * pi, 2 * pi + 1)
+    if RF and pi == RP:
+        pair = (2 * pi + 1, 2 * pi)
+    return tuple((c, "R" if (R0 <= T < RL and c == 2 * RP + 1) else "F") for c in pair)
 
 
 def XLIM(q):
@@ -35,35 +40,46 @@ ALU = mybir.AluOpType
 P = 128
 NG = 8
 NU = 32
-VE = (3,)
-XA = (6, 8, 9)
-WA = (7, 9, 10)
+VE = ()
+XA = (6, 7, 8)
+WA = (6, 8, 8)
 XB = -1
 WB = 2
-ORD = 1
+ORD = 0
 SEQ = [(0, 0), (0, 1), (0, 2), (0, 3), (1, 0), (1, 1), (1, 2), (1, 3)] if ORD == 0 else [(0, 0), (0, 1), (0, 2), (1, 0), (1, 1), (1, 2), (0, 3), (1, 3)] if ORD == 1 else [(0, 0), (0, 1), (1, 0), (1, 1), (0, 2), (1, 2), (0, 3), (1, 3)]
 SEQ = SEQ + [(t, p) for t in range(2, 8) for p in range(4)]
 WAT = (0, 1, 2)
 EVN = ()
 EVE = "S"
-WC = ('V', 'V', 'V', 'S')
+WC = ('V', 'V', 'V', 'V')
 ST = 2
 TB = 1
 LASTV = 0
-LASTS = ((0, 4), (1, 2), (3, 5), (6, 7))
+LASTS = ((0, 4), (1, 5), (2, 3), (6, 7))
 LASTR = (3, 4, 5, 6, 7)
-RP = 3
-R0 = 9
-HEAD = 1
-EV3 = 'S'
+RP = 2
+R0 = 2
+SH = 2
+TG = {"xt": "xt", "acc": "acc", "fl": "fl", "ot_ps": "ot_ps"} if SH == 0 else {"xt": "ox", "acc": "acc", "fl": "fl", "ot_ps": "ox"} if SH == 1 else {"xt": "b", "acc": "b", "fl": "b", "ot_ps": "b"} if SH == 2 else {"xt": "ox", "acc": "af", "fl": "af", "ot_ps": "ox"} if SH == 3 else {"xt": "xt", "acc": "b", "fl": "b", "ot_ps": "b"}
+BF = {"xt": 2, "acc": 2, "fl": 2, "ot_ps": 2} if SH == 0 else {"xt": 4, "acc": 2, "fl": 2, "ot_ps": 4} if SH == 1 else {"xt": 8, "acc": 8, "fl": 8, "ot_ps": 8} if SH == 2 else {"xt": 4, "acc": 4, "fl": 4, "ot_ps": 4} if SH == 3 else {"xt": 1, "acc": 7, "fl": 7, "ot_ps": 7}
+RSKEW = 1
+PENR = (6, 7)
+PENS = ((0, 4), (1, 5), (2, 6), (3, 7))
+RF = 0
+RL = 6
+IE = ("S", "S", "S", "S")
+OV = (1,)
+WBP = 0
+HEAD = 0
+EV3 = 'V'
 W4 = 0
-WPOS = (0, 1)
-QV = 4
+WPOS = (1, 2)
+QV = 8
 QL = 99
-QE = 99
+QE = 4
 IT = (3, 10, 18)
 QA = 0
-FIRST_ORDERED = 12
+FIRST_ORDERED = 99
 NQ = 32
 
 
@@ -197,7 +213,7 @@ def tile_splatinformationflow_pb_kernel(tc, x_bytes, x_scale, infl, dec, gate_w,
 
         def x_transpose(m):
             T, j = m // 4, m % 4
-            xt_t = psum.tile([P, 2, 2, 128], F32, name="xt", tag="xt", bufs=2)
+            xt_t = psum.tile([P, 2, 2, 128], F32, name="xt", tag=TG["xt"], bufs=BF["xt"])
             xt[m] = xt_t
             words = xw[T][:].rearrange("p j k -> p (j k)").bitcast(F32)
             for g in range(2):
@@ -244,13 +260,16 @@ def tile_splatinformationflow_pb_kernel(tc, x_bytes, x_scale, infl, dec, gate_w,
                 )
 
         def infl_transpose(b):
-            it = psum.tile([P, 8, 128], BF16, name="it", tag="xt", bufs=2)
+            it = psum.tile([P, 8, 128], BF16, name="it", tag=TG["xt"], bufs=BF["xt"])
             for j in range(8):
                 nc.tensor.transpose(it[:, j, :], inf[:, b, j, :], ident_b[:])
-            nc.scalar.copy(out=inflT[:, 1024 * b:1024 * (b + 1)], in_=it[:].rearrange("p j r -> p (j r)"))
+            if IE[b] == "S":
+                nc.scalar.copy(out=inflT[:, 1024 * b:1024 * (b + 1)], in_=it[:].rearrange("p j r -> p (j r)"))
+            else:
+                nc.vector.tensor_copy(out=inflT[:, 1024 * b:1024 * (b + 1)], in_=it[:].rearrange("p j r -> p (j r)"))
 
         def gate_mm(T, c):
-            acc_t = psum.tile([P, 512], F32, name="acc", tag="acc", bufs=2)
+            acc_t = psum.tile([P, 512], F32, name="acc", tag=TG["acc"], bufs=BF["acc"])
             acc[c] = acc_t
             for g in range(2):
                 nc.tensor.matmul_mx(
@@ -269,7 +288,7 @@ def tile_splatinformationflow_pb_kernel(tc, x_bytes, x_scale, infl, dec, gate_w,
             nc.scalar.activation(out=gt_t[:], in_=acc[c][:], func=ACT.Sigmoid, bias=bias[:, c:c + 1], scale=1.0)
 
         def flow_mm(T, c):
-            fl_t = psum.tile([P, 512], F32, name="fl", tag="fl", bufs=2)
+            fl_t = psum.tile([P, 512], F32, name="fl", tag=TG["fl"], bufs=BF["fl"])
             fl[c] = fl_t
             nc.tensor.matmul(
                 fl_t[:], lhsT=dc[:, T // 2, 128 * c:128 * (c + 1)], rhs=inflT[:, 512 * T:512 * (T + 1)],
@@ -282,7 +301,7 @@ def tile_splatinformationflow_pb_kernel(tc, x_bytes, x_scale, infl, dec, gate_w,
             nc.vector.tensor_tensor(out=ot_t[:], in0=fl[c][:], in1=gt[c][:], op=ALU.mult)
 
         def o_transpose(T, c, tag="ot_ps"):
-            ps = psum.tile([P, 4, 128], F32, name="ot_ps", tag=tag, bufs=2)
+            ps = psum.tile([P, 4, 128], F32, name="ot_ps", tag=TG[tag], bufs=BF[tag])
             ot_ps[(T, c)] = ps
             for j in range(4):
                 nc.tensor.transpose(ps[:, j, :], ot_sb[(T, c)][:, 128 * j:128 * (j + 1)], ident_f[:])
@@ -295,7 +314,7 @@ def tile_splatinformationflow_pb_kernel(tc, x_bytes, x_scale, infl, dec, gate_w,
                 nc.vector.tensor_copy(out=o_sb[T][:, :, 128 * c:128 * (c + 1)], in_=ot_ps[(T, c)][:])
 
         def row_mm(T, c):
-            z_t = psum.tile([P, 4, 128], F32, name="acc", tag="acc", bufs=2)
+            z_t = psum.tile([P, 4, 128], F32, name="acc", tag=TG["acc"], bufs=BF["acc"])
             acc[c] = z_t
             lo = 128 * (c % 2)
             for j in range(4):
@@ -324,7 +343,7 @@ def tile_splatinformationflow_pb_kernel(tc, x_bytes, x_scale, infl, dec, gate_w,
             gt[c] = g_t
 
         def row_flow(T, c):
-            fl_t = psum.tile([P, 4, 128], F32, name="fl", tag="fl", bufs=2)
+            fl_t = psum.tile([P, 4, 128], F32, name="fl", tag=TG["fl"], bufs=BF["fl"])
             fl[c] = fl_t
             for j in range(4):
                 lo = 512 * T + 128 * j
@@ -350,7 +369,7 @@ def tile_splatinformationflow_pb_kernel(tc, x_bytes, x_scale, infl, dec, gate_w,
                 in_=o_sb[T][:, :, 128 * c_lo:128 * c_hi],
             )
 
-        bt = psum.tile([P, P], BF16, name="bt", tag="acc", bufs=2)
+        bt = psum.tile([P, P], BF16, name="bt", tag=TG["acc"], bufs=BF["acc"])
         nc.tensor.transpose(bt[:], brows[:], ident_b[:])
         if HEAD == 0:
             for m in range(4):
@@ -401,6 +420,7 @@ def tile_splatinformationflow_pb_kernel(tc, x_bytes, x_scale, infl, dec, gate_w,
                 widen(4)
         n_wide, n_tr, n_ev, n_quant = 5, 4, 4, 1
 
+        pend = []
         for q in range(0, NQ + 1):
             T = q // 4
             slots = SLOT(q)
@@ -425,9 +445,19 @@ def tile_splatinformationflow_pb_kernel(tc, x_bytes, x_scale, infl, dec, gate_w,
                 if form == "R":
                     row_add(c)
             for c, form in slots:
-                (sigmoid if form == "F" else row_sigmoid)(c)
+                if form == "F":
+                    sigmoid(c)
+            if RSKEW == 0:
+                for c, form in slots:
+                    if form == "R":
+                        row_sigmoid(c)
             for c, form in slots:
-                (flow_mm if form == "F" else row_flow)(T, c)
+                if form == "F":
+                    flow_mm(T, c)
+            now = [(T, c) for c, form in slots if form == "R"]
+            todo = now if RSKEW == 0 else pend
+            for TT, c in todo:
+                row_flow(TT, c)
             for e in late:
                 x_evac("S", e)
             for i in range(1, 4):
@@ -439,11 +469,12 @@ def tile_splatinformationflow_pb_kernel(tc, x_bytes, x_scale, infl, dec, gate_w,
                 n_quant += 1
                 doq = False
             for c, form in slots:
-                (product if form == "F" else row_product)(T, c)
-            if q >= 28:
-                for c, form in slots:
-                    if form == "R":
-                        store(T, c, c + 1)
+                if form == "F":
+                    product(T, c)
+            for TT, c in todo:
+                row_product(TT, c)
+                if TT == NG - 1 or (PENR and TT == NG - 2):
+                    store(TT, c, c + 1)
             for c, form in prev:
                 if form == "F":
                     o_transpose(Tp, c, "xt" if q == NQ else "ot_ps")
@@ -459,11 +490,15 @@ def tile_splatinformationflow_pb_kernel(tc, x_bytes, x_scale, infl, dec, gate_w,
                 doq = n_quant < NG and n_ev >= 4 * n_quant + 4
             for s, (c, form) in enumerate(prev):
                 if form == "F":
-                    o_evac("V" if s == 1 and q >= 29 and LASTV else "S", Tp, c)
-                    if Tp == NG - 1:
+                    o_evac("V" if (s == 1 and q >= 29 and LASTV) or (s == 1 and q % 8 in OV and q >= 8) else "S", Tp, c)
+                    if Tp == NG - 1 or (PENR and Tp == NG - 2):
                         store(Tp, c, c + 1)
-            if q >= 1 and Tp < NG - 1 and (q - 1) % 2 == 1:
+            if q >= 1 and Tp < (NG - 2 if PENR else NG - 1) and (q - 1) % 2 == 1:
                 store(Tp, 4 * ((q - 1) % 4 // 2), 4 * ((q - 1) % 4 // 2) + 4)
+            if RSKEW:
+                for TT, c in now:
+                    row_sigmoid(c)
+            pend = now
             if q in IT:
                 infl_transpose(IT.index(q) + 1)
             if doq and QA == 0:

@@ -8,14 +8,7 @@ def SLOT(q):
     if q < 0 or q >= 32:
         return ()
     T, pi = q // 4, q % 4
-    if T == 7:
-        return tuple((c, "R" if c in LASTR else "F") for c in LASTS[pi])
-    if T == 6 and PENR:
-        return tuple((c, "R" if c in PENR else "F") for c in PENS[pi])
-    pair = (2 * pi, 2 * pi + 1)
-    if RF and pi == RP:
-        pair = (2 * pi + 1, 2 * pi)
-    return tuple((c, "R" if (R0 <= T < RL and c == 2 * RP + 1) else "F") for c in pair)
+    return GS[GK[T]][pi]
 
 
 def XLIM(q):
@@ -43,7 +36,7 @@ NU = 32
 VE = ()
 XA = (6, 7, 8)
 WA = (6, 8, 8)
-XB = -1
+XB = -2
 WB = 2
 ORD = 0
 SEQ = [(0, 0), (0, 1), (0, 2), (0, 3), (1, 0), (1, 1), (1, 2), (1, 3)] if ORD == 0 else [(0, 0), (0, 1), (0, 2), (1, 0), (1, 1), (1, 2), (0, 3), (1, 3)] if ORD == 1 else [(0, 0), (0, 1), (1, 0), (1, 1), (0, 2), (1, 2), (0, 3), (1, 3)]
@@ -55,31 +48,42 @@ WC = ('V', 'V', 'V', 'V')
 ST = 2
 TB = 1
 LASTV = 0
-LASTS = ((0, 4), (1, 5), (2, 3), (6, 7))
-LASTR = (3, 4, 5, 6, 7)
-RP = 2
-R0 = 2
+LASTS = ((0, 4), (1, 2), (3, 5), (6, 7))
+LASTR = (4, 5, 6, 7)
+RP = 3
+R0 = 1
+NOORD = ()
+GK = (0, 0, 1, 0, 1, 1, 2, 3)
+GS0 = (((0, "F"), (1, "F")), ((2, "F"), (3, "F")), ((4, "F"), (5, "F")), ((6, "F"), (7, "F")))
+GS1 = (((0, "F"), (1, "F")), ((2, "F"), (3, "F")), ((4, "F"), ((3, 0), "R")), ((5, "F"), ((3, 1), "R")))
+GS2 = (((0, "F"), ((2, 0), "R")), ((1, "F"), ((2, 1), "R")), ((2, "F"), ((3, 0), "R")), ((3, "F"), ((3, 1), "R")))
+GS3 = (((0, "F"), ((1, 0), "R")), ((1, "F"), ((1, 1), "R")), (((2, 0), "R"), ((2, 1), "R")), (((3, 0), "R"), ((3, 1), "R")))
+GS4 = (((0, "F"), ((3, 0), "R")), ((1, "F"), ((3, 1), "R")), ((2, "F"), (3, "F")), ((4, "F"), (5, "F")))
+GS5 = (((0, "F"), ((2, 0), "R")), ((1, "F"), (2, "F")), ((3, "F"), ((2, 1), "R")), (((3, 0), "R"), ((3, 1), "R")))
+GS = (GS0, GS1, GS2, GS3, GS4, GS5)
+RC = (5,)
+TO = 0
 SH = 2
 TG = {"xt": "xt", "acc": "acc", "fl": "fl", "ot_ps": "ot_ps"} if SH == 0 else {"xt": "ox", "acc": "acc", "fl": "fl", "ot_ps": "ox"} if SH == 1 else {"xt": "b", "acc": "b", "fl": "b", "ot_ps": "b"} if SH == 2 else {"xt": "ox", "acc": "af", "fl": "af", "ot_ps": "ox"} if SH == 3 else {"xt": "xt", "acc": "b", "fl": "b", "ot_ps": "b"}
 BF = {"xt": 2, "acc": 2, "fl": 2, "ot_ps": 2} if SH == 0 else {"xt": 4, "acc": 2, "fl": 2, "ot_ps": 4} if SH == 1 else {"xt": 8, "acc": 8, "fl": 8, "ot_ps": 8} if SH == 2 else {"xt": 4, "acc": 4, "fl": 4, "ot_ps": 4} if SH == 3 else {"xt": 1, "acc": 7, "fl": 7, "ot_ps": 7}
 RSKEW = 1
-PENR = (6, 7)
+PENR = (4, 5, 6, 7)
 PENS = ((0, 4), (1, 5), (2, 6), (3, 7))
 RF = 0
-RL = 6
+RL = 7
 IE = ("S", "S", "S", "S")
-OV = (1,)
+OV = ()
 WBP = 0
 HEAD = 0
-EV3 = 'V'
+EV3 = 'S'
 W4 = 0
-WPOS = (1, 2)
-QV = 8
+WPOS = (0, 2)
+QV = 12
 QL = 99
 QE = 4
-IT = (3, 10, 18)
+IT = (3, 10, 17)
 QA = 0
-FIRST_ORDERED = 99
+FIRST_ORDERED = 16
 NQ = 32
 
 
@@ -219,7 +223,7 @@ def tile_splatinformationflow_pb_kernel(tc, x_bytes, x_scale, infl, dec, gate_w,
             for g in range(2):
                 for u in range(2):
                     lo = 512 * j + 256 * g
-                    src = xp[T][:, j, g, u, :] if m >= FIRST_ORDERED else words[:, lo + u:lo + 256:2]
+                    src = xp[T][:, j, g, u, :] if m >= FIRST_ORDERED and m % 4 not in NOORD else words[:, lo + u:lo + 256:2]
                     nc.tensor.transpose(xt_t[:, g, u, :], src, ident_f[:])
 
         def x_evac(eng, m):
@@ -283,7 +287,7 @@ def tile_splatinformationflow_pb_kernel(tc, x_bytes, x_scale, infl, dec, gate_w,
                 )
 
         def sigmoid(c):
-            gt_t = work.tile([P, 512], F32, name="gt", tag="gt", bufs=3)
+            gt_t = work.tile([P, 512], F32, name="gt", tag="gt", bufs=4)
             gt[c] = gt_t
             nc.scalar.activation(out=gt_t[:], in_=acc[c][:], func=ACT.Sigmoid, bias=bias[:, c:c + 1], scale=1.0)
 
@@ -314,41 +318,44 @@ def tile_splatinformationflow_pb_kernel(tc, x_bytes, x_scale, infl, dec, gate_w,
                 nc.vector.tensor_copy(out=o_sb[T][:, :, 128 * c:128 * (c + 1)], in_=ot_ps[(T, c)][:])
 
         def row_mm(T, c):
-            z_t = psum.tile([P, 4, 128], F32, name="acc", tag=TG["acc"], bufs=BF["acc"])
+            i, h = c
+            z_t = psum.tile([P, 2, 256], F32, name="acc", tag=TG["acc"], bufs=BF["acc"])
             acc[c] = z_t
-            lo = 128 * (c % 2)
-            for j in range(4):
+            for jj in range(2):
                 for g in range(2):
+                    lo = 128 * (2 * h + jj)
                     nc.tensor.matmul_mx(
-                        out=z_t[:, j, :],
-                        lhsT=xc[T][:, g, 128 * j:128 * (j + 1)].bitcast(FP8X4),
-                        lhsT_scale=xs[T][:, g, 128 * j:128 * (j + 1)],
-                        rhs=wc[:, c // 2, g, lo:lo + 128].bitcast(FP8X4),
-                        rhs_scale=ws[:, c // 2, g, lo:lo + 128],
+                        out=z_t[:, jj, :],
+                        lhsT=xc[T][:, g, lo:lo + 128].bitcast(FP8X4),
+                        lhsT_scale=xs[T][:, g, lo:lo + 128],
+                        rhs=wc[:, i, g, :].bitcast(FP8X4),
+                        rhs_scale=ws[:, i, g, :],
                         start=(g == 0),
                         stop=(g == 1),
                     )
 
         def row_add(c):
-            zb_t = work.tile([P, 4, 128], F32, name="zb", tag="zb", bufs=2)
+            i, h = c
+            zb_t = work.tile([P, 2, 256], F32, name="zb", tag="zb", bufs=2)
             gt[c] = zb_t
             nc.vector.tensor_tensor(
                 out=zb_t[:], in0=acc[c][:],
-                in1=brow[:, 128 * c:128 * (c + 1)].unsqueeze(1).to_broadcast([P, 4, 128]), op=ALU.add,
+                in1=brow[:, 256 * i:256 * (i + 1)].unsqueeze(1).to_broadcast([P, 2, 256]), op=ALU.add,
             )
 
         def row_sigmoid(c):
-            g_t = work.tile([P, 4, 128], F32, name="gt", tag="gt", bufs=3)
+            g_t = work.tile([P, 2, 256], F32, name="gt", tag="gt", bufs=4)
             nc.scalar.activation(out=g_t[:], in_=gt[c][:], func=ACT.Sigmoid)
             gt[c] = g_t
 
         def row_flow(T, c):
-            fl_t = psum.tile([P, 4, 128], F32, name="fl", tag=TG["fl"], bufs=BF["fl"])
+            i, h = c
+            fl_t = psum.tile([P, 2, 256], F32, name="fl", tag=TG["fl"], bufs=BF["fl"])
             fl[c] = fl_t
-            for j in range(4):
-                lo = 512 * T + 128 * j
+            for jj in range(2):
+                lo = 512 * T + 128 * (2 * h + jj)
                 nc.tensor.matmul(
-                    fl_t[:, j, :], lhsT=inflT[:, lo:lo + 128], rhs=dc[:, T // 2, 128 * c:128 * (c + 1)],
+                    fl_t[:, jj, :], lhsT=inflT[:, lo:lo + 128], rhs=dc[:, T // 2, 256 * i:256 * (i + 1)],
                     start=True, stop=True,
                 )
 
@@ -359,8 +366,16 @@ def tile_splatinformationflow_pb_kernel(tc, x_bytes, x_scale, infl, dec, gate_w,
             return o_sb[T]
 
         def row_product(T, c):
+            i, h = c
             nc.vector.tensor_tensor(
-                out=o_tile(T)[:, :, 128 * c:128 * (c + 1)], in0=fl[c][:], in1=gt[c][:], op=ALU.mult,
+                out=o_tile(T)[:, 2 * h:2 * h + 2, 256 * i:256 * (i + 1)], in0=fl[c][:], in1=gt[c][:], op=ALU.mult,
+            )
+
+        def row_store(T, c):
+            i, h = c
+            nc.sync.dma_start(
+                out=out_view[T // 2, T % 2][:, 2 * h:2 * h + 2, 256 * i:256 * (i + 1)],
+                in_=o_sb[T][:, 2 * h:2 * h + 2, 256 * i:256 * (i + 1)],
             )
 
         def store(T, c_lo, c_hi):
@@ -428,7 +443,7 @@ def tile_splatinformationflow_pb_kernel(tc, x_bytes, x_scale, infl, dec, gate_w,
             Tp = (q - 1) // 4
             late = []
             while n_ev < n_tr:
-                if q >= QV and q % 4 in VE:
+                if q >= QV and q % 8 in VE:
                     x_evac("V", n_ev)
                 elif q >= QL:
                     late.append(n_ev)
@@ -439,8 +454,38 @@ def tile_splatinformationflow_pb_kernel(tc, x_bytes, x_scale, infl, dec, gate_w,
                 if q == WAT[i - 1]:
                     w_copy("S", i, 0)
                     w_copy(WC[i], i, 1)
-            for c, form in slots:
-                (gate_mm if form == "F" else row_mm)(T, c)
+            now = [(T, c) for c, form in slots if form == "R"]
+            todo = now if RSKEW == 0 else pend
+            if TO == 0:
+                for c, form in slots:
+                    (gate_mm if form == "F" else row_mm)(T, c)
+                for c, form in slots:
+                    if form == "F":
+                        flow_mm(T, c)
+                for TT, c in todo:
+                    row_flow(TT, c)
+            elif TO == 1:
+                for c, form in slots:
+                    (gate_mm if form == "F" else row_mm)(T, c)
+                    if form == "F":
+                        flow_mm(T, c)
+                for TT, c in todo:
+                    row_flow(TT, c)
+            elif TO == 3:
+                for TT, c in todo:
+                    row_flow(TT, c)
+                for c, form in slots:
+                    if form == "F":
+                        flow_mm(T, c)
+                for c, form in slots:
+                    (gate_mm if form == "F" else row_mm)(T, c)
+            else:
+                for TT, c in todo:
+                    row_flow(TT, c)
+                for c, form in slots:
+                    if form == "F":
+                        flow_mm(T, c)
+                    (gate_mm if form == "F" else row_mm)(T, c)
             for c, form in slots:
                 if form == "R":
                     row_add(c)
@@ -451,13 +496,6 @@ def tile_splatinformationflow_pb_kernel(tc, x_bytes, x_scale, infl, dec, gate_w,
                 for c, form in slots:
                     if form == "R":
                         row_sigmoid(c)
-            for c, form in slots:
-                if form == "F":
-                    flow_mm(T, c)
-            now = [(T, c) for c, form in slots if form == "R"]
-            todo = now if RSKEW == 0 else pend
-            for TT, c in todo:
-                row_flow(TT, c)
             for e in late:
                 x_evac("S", e)
             for i in range(1, 4):
@@ -473,8 +511,7 @@ def tile_splatinformationflow_pb_kernel(tc, x_bytes, x_scale, infl, dec, gate_w,
                     product(T, c)
             for TT, c in todo:
                 row_product(TT, c)
-                if TT == NG - 1 or (PENR and TT == NG - 2):
-                    store(TT, c, c + 1)
+                row_store(TT, c)
             for c, form in prev:
                 if form == "F":
                     o_transpose(Tp, c, "xt" if q == NQ else "ot_ps")
@@ -491,10 +528,15 @@ def tile_splatinformationflow_pb_kernel(tc, x_bytes, x_scale, infl, dec, gate_w,
             for s, (c, form) in enumerate(prev):
                 if form == "F":
                     o_evac("V" if (s == 1 and q >= 29 and LASTV) or (s == 1 and q % 8 in OV and q >= 8) else "S", Tp, c)
-                    if Tp == NG - 1 or (PENR and Tp == NG - 2):
+                    if GK[Tp] > 1:
                         store(Tp, c, c + 1)
-            if q >= 1 and Tp < (NG - 2 if PENR else NG - 1) and (q - 1) % 2 == 1:
-                store(Tp, 4 * ((q - 1) % 4 // 2), 4 * ((q - 1) % 4 // 2) + 4)
+            if prev and GK[Tp] < 2:
+                fs = [c for c, form in prev if form == "F"]
+                if Tp < NG - 1 and GK[Tp] == 0:
+                    if (q - 1) % 2 == 1:
+                        store(Tp, fs[-1] - 3, fs[-1] + 1)
+                elif len(fs) == 2 or fs[0] % 2 == 1:
+                    store(Tp, fs[-1] - 1, fs[-1] + 1)
             if RSKEW:
                 for TT, c in now:
                     row_sigmoid(c)
@@ -508,7 +550,7 @@ def tile_splatinformationflow_pb_kernel(tc, x_bytes, x_scale, infl, dec, gate_w,
             started = 0
             while n_wide < min(NU, WLIM(q)) and started < ST:
                 widen(n_wide)
-                if n_wide >= FIRST_ORDERED:
+                if n_wide >= FIRST_ORDERED and n_wide % 4 not in NOORD:
                     x_order(n_wide)
                 n_wide += 1
                 started += 1

@@ -12,11 +12,11 @@ def SLOT(q):
 
 
 def XLIM(q):
-    return XA[q] if q < len(XA) else max(XA[-1], q + 6 - XB)
+    return XA[q] if q < len(XA) else max(XA[-1], q + 6 - XB + (q >= LG[0]) + (q >= LG[1]))
 
 
 def WLIM(q):
-    return WA[q] if q < len(WA) else max(WA[-1], q + 6 - XB + WB)
+    return WA[q] if q < len(WA) else max(WA[-1], q + 6 - XB + WB + (q >= LG[0]) + (q >= LG[1]))
 
 
 FLOPS = 2 * B * S * D * D + 2 * B * S * KS * D
@@ -34,9 +34,9 @@ P = 128
 NG = 8
 NU = 32
 VE = ()
-XA = (6, 7, 8)
-WA = (6, 8, 8)
-XB = -2
+XA = (6, 8, 9)
+WA = (7, 9, 10)
+XB = -1
 WB = 2
 ORD = 0
 SEQ = [(0, 0), (0, 1), (0, 2), (0, 3), (1, 0), (1, 1), (1, 2), (1, 3)] if ORD == 0 else [(0, 0), (0, 1), (0, 2), (1, 0), (1, 1), (1, 2), (0, 3), (1, 3)] if ORD == 1 else [(0, 0), (0, 1), (1, 0), (1, 1), (0, 2), (1, 2), (0, 3), (1, 3)]
@@ -44,7 +44,7 @@ SEQ = SEQ + [(t, p) for t in range(2, 8) for p in range(4)]
 WAT = (0, 1, 2)
 EVN = ()
 EVE = "S"
-WC = ('V', 'V', 'V', 'V')
+WC = ('V', 'V', 'V', 'S')
 ST = 2
 TB = 1
 LASTV = 0
@@ -52,15 +52,20 @@ LASTS = ((0, 4), (1, 2), (3, 5), (6, 7))
 LASTR = (4, 5, 6, 7)
 RP = 3
 R0 = 1
-NOORD = ()
-GK = (0, 0, 1, 0, 1, 1, 2, 3)
+LG = (99, 99)
+NOORD = (1, 3)
+GK = (0, 1, 0, 1, 0, 1, 5, 7)
 GS0 = (((0, "F"), (1, "F")), ((2, "F"), (3, "F")), ((4, "F"), (5, "F")), ((6, "F"), (7, "F")))
 GS1 = (((0, "F"), (1, "F")), ((2, "F"), (3, "F")), ((4, "F"), ((3, 0), "R")), ((5, "F"), ((3, 1), "R")))
 GS2 = (((0, "F"), ((2, 0), "R")), ((1, "F"), ((2, 1), "R")), ((2, "F"), ((3, 0), "R")), ((3, "F"), ((3, 1), "R")))
 GS3 = (((0, "F"), ((1, 0), "R")), ((1, "F"), ((1, 1), "R")), (((2, 0), "R"), ((2, 1), "R")), (((3, 0), "R"), ((3, 1), "R")))
 GS4 = (((0, "F"), ((3, 0), "R")), ((1, "F"), ((3, 1), "R")), ((2, "F"), (3, "F")), ((4, "F"), (5, "F")))
 GS5 = (((0, "F"), ((2, 0), "R")), ((1, "F"), (2, "F")), ((3, "F"), ((2, 1), "R")), (((3, 0), "R"), ((3, 1), "R")))
-GS = (GS0, GS1, GS2, GS3, GS4, GS5)
+GS6 = ((((3, 0), "R"), ((3, 1), "R")), (((2, 0), "R"), ((2, 1), "R")), ((0, "F"), (1, "F")), ((2, "F"), (3, "F")))
+GS7 = (((0, "F"), ((2, 0), "R")), ((1, "F"), ((2, 1), "R")), ((2, "F"), (3, "F")), (((3, 0), "R"), ((3, 1), "R")))
+GS8 = (((0, "F"), ((3, 0), "R")), ((1, "F"), (2, "F")), ((3, "F"), ((3, 1), "R")), ((4, "F"), (5, "F")))
+GS9 = (((0, "F"), ((2, 0), "R")), ((1, "F"), ((2, 1), "R")), ((2, "F"), ((3, 0), "R")), (((3, 1), "R"), (3, "F")))
+GS = (GS0, GS1, GS2, GS3, GS4, GS5, GS6, GS7, GS8, GS9)
 RC = (5,)
 TO = 0
 SH = 2
@@ -74,16 +79,16 @@ RL = 7
 IE = ("S", "S", "S", "S")
 OV = ()
 WBP = 0
-HEAD = 0
+HEAD = 1
 EV3 = 'S'
 W4 = 0
 WPOS = (0, 2)
 QV = 12
 QL = 99
 QE = 4
-IT = (3, 10, 17)
+IT = (6, 14, 22)
 QA = 0
-FIRST_ORDERED = 16
+FIRST_ORDERED = 12
 NQ = 32
 
 
@@ -471,6 +476,31 @@ def tile_splatinformationflow_pb_kernel(tc, x_bytes, x_scale, infl, dec, gate_w,
                         flow_mm(T, c)
                 for TT, c in todo:
                     row_flow(TT, c)
+            elif TO == 5:
+                gate_first = [c for c, form in slots if form == "F"]
+                for c in gate_first[:1]:
+                    gate_mm(T, c)
+                for c in gate_first:
+                    flow_mm(T, c)
+                for TT, c in todo:
+                    row_flow(TT, c)
+                for c, form in slots:
+                    if form == "R":
+                        row_mm(T, c)
+                    elif c not in gate_first[:1]:
+                        gate_mm(T, c)
+            elif TO == 6:
+                for c, form in slots:
+                    if form == "F":
+                        gate_mm(T, c)
+                for c, form in slots:
+                    if form == "F":
+                        flow_mm(T, c)
+                for TT, c in todo:
+                    row_flow(TT, c)
+                for c, form in slots:
+                    if form == "R":
+                        row_mm(T, c)
             elif TO == 3:
                 for TT, c in todo:
                     row_flow(TT, c)

@@ -52,6 +52,8 @@ LASTS = ((0, 4), (1, 2), (3, 5), (6, 7))
 LASTR = (4, 5, 6, 7)
 RP = 3
 R0 = 1
+WLOAD = 256
+ALB = 256
 LG = (99, 99)
 NOORD = (1, 3)
 GK = (0, 1, 0, 1, 0, 1, 5, 7)
@@ -65,7 +67,12 @@ GS6 = ((((3, 0), "R"), ((3, 1), "R")), (((2, 0), "R"), ((2, 1), "R")), ((0, "F")
 GS7 = (((0, "F"), ((2, 0), "R")), ((1, "F"), ((2, 1), "R")), ((2, "F"), (3, "F")), (((3, 0), "R"), ((3, 1), "R")))
 GS8 = (((0, "F"), ((3, 0), "R")), ((1, "F"), (2, "F")), ((3, "F"), ((3, 1), "R")), ((4, "F"), (5, "F")))
 GS9 = (((0, "F"), ((2, 0), "R")), ((1, "F"), ((2, 1), "R")), ((2, "F"), ((3, 0), "R")), (((3, 1), "R"), (3, "F")))
-GS = (GS0, GS1, GS2, GS3, GS4, GS5, GS6, GS7, GS8, GS9)
+GS10 = ((((2, 0), "R"), ((2, 1), "R")), ((0, "F"), (1, "F")), ((2, "F"), ((3, 0), "R")), ((3, "F"), ((3, 1), "R")))
+GS11 = (((0, "F"), ((2, 0), "R")), (((2, 1), "R"), (1, "F")), (((3, 0), "R"), ((3, 1), "R")), ((2, "F"), (3, "F")))
+GS12 = (((0, "F"), (1, "F")), ((2, "F"), ((2, 0), "R")), ((3, "F"), ((2, 1), "R")), (((3, 0), "R"), ((3, 1), "R")))
+GS13 = (((0, "F"), ((1, 0), "R")), ((1, "F"), ((1, 1), "R")), (((2, 0), "R"), ((2, 1), "R")), (((3, 0), "R"), ((3, 1), "R")))
+GS14 = (((0, "F"), (1, "F")), ((2, "F"), ((3, 0), "R")), ((3, "F"), ((3, 1), "R")), ((4, "F"), (5, "F")))
+GS = (GS0, GS1, GS2, GS3, GS4, GS5, GS6, GS7, GS8, GS9, GS10, GS11, GS12, GS13, GS14)
 RC = (5,)
 TO = 0
 SH = 2
@@ -112,9 +119,9 @@ def tile_splatinformationflow_pb_kernel(tc, x_bytes, x_scale, infl, dec, gate_w,
             xb.append(xb_t)
         sc = keep.tile([P, 1024], F32, name="sc")
         wr = keep.tile([P, 2, 4, 1024], BF16, name="wr")
-        wg = keep.tile([P, 4, 2, 1024], BF16, name="wg", align_bytes=64)
-        wc = keep.tile([P, 4, 2, 256], U32, name="wc", align_bytes=64)
-        ws = keep.tile([P, 4, 2, 256], U8, name="ws", align_bytes=64)
+        wg = keep.tile([P, 4, 2, 1024], BF16, name="wg", align_bytes=ALB)
+        wc = keep.tile([P, 4, 2, 256], U32, name="wc", align_bytes=ALB)
+        ws = keep.tile([P, 4, 2, 256], U8, name="ws", align_bytes=ALB)
         inf = keep.tile([P, 4, 8, 128], BF16, name="inf")
         inflT = keep.tile([P, 4096], BF16, name="inflT")
         dc = keep.tile([P, 4, 1024], BF16, name="dc")
@@ -151,10 +158,11 @@ def tile_splatinformationflow_pb_kernel(tc, x_bytes, x_scale, infl, dec, gate_w,
             for j in range(4):
                 load_x_unit(0, j)
                 if j in WPOS:
-                    load_w(WPOS.index(j), 0, 256)
+                    load_w(WPOS.index(j), 0, WLOAD)
         load_flow(0)
-        load_w(0, 256, 512)
-        load_w(1, 256, 512)
+        if WLOAD == 256:
+            load_w(0, 256, 512)
+            load_w(1, 256, 512)
         load_x(1)
         load_w(0, 512, 1024)
         load_w(1, 512, 1024)
@@ -234,7 +242,7 @@ def tile_splatinformationflow_pb_kernel(tc, x_bytes, x_scale, infl, dec, gate_w,
         def x_evac(eng, m):
             T, j = m // 4, m % 4
             if j == 0:
-                gr_t = work.tile([P, 2, 2048], BF16, name="gr", tag="gr", bufs=2, align_bytes=64)
+                gr_t = work.tile([P, 2, 2048], BF16, name="gr", tag="gr", bufs=2, align_bytes=ALB)
                 gr[T] = gr_t
             gw = gr[T][:].rearrange("p g c -> p (g c)").bitcast(F32).rearrange("p (g r u) -> p g r u", g=2, u=2)
             dst = gw[:, :, 128 * j:128 * (j + 1), :]
@@ -245,8 +253,8 @@ def tile_splatinformationflow_pb_kernel(tc, x_bytes, x_scale, infl, dec, gate_w,
                 nc.vector.tensor_copy(out=dst, in_=src)
 
         def x_quant(T):
-            xc_t = work.tile([P, 2, 512], U32, name="xc", tag="xc", bufs=3, align_bytes=64)
-            xs_t = work.tile([P, 2, 512], U8, name="xs", tag="xs", bufs=3, align_bytes=64)
+            xc_t = work.tile([P, 2, 512], U32, name="xc", tag="xc", bufs=3, align_bytes=ALB)
+            xs_t = work.tile([P, 2, 512], U8, name="xs", tag="xs", bufs=3, align_bytes=ALB)
             xc[T] = xc_t
             xs[T] = xs_t
             nc.vector.quantize_mx(
@@ -257,8 +265,8 @@ def tile_splatinformationflow_pb_kernel(tc, x_bytes, x_scale, infl, dec, gate_w,
 
         def x_quant_half(T, half):
             if half == 0:
-                xc_t = work.tile([P, 2, 512], U32, name="xc", tag="xc", bufs=3, align_bytes=64)
-                xs_t = work.tile([P, 2, 512], U8, name="xs", tag="xs", bufs=3, align_bytes=64)
+                xc_t = work.tile([P, 2, 512], U32, name="xc", tag="xc", bufs=3, align_bytes=ALB)
+                xs_t = work.tile([P, 2, 512], U8, name="xs", tag="xs", bufs=3, align_bytes=ALB)
                 xc[T] = xc_t
                 xs[T] = xs_t
             for g in range(2):

@@ -115,22 +115,22 @@ def tile_splatinformationflow_pb_kernel(tc, x_bytes, x_scale, infl, dec, gate_w,
 
         xb = []
         for T in range(NG):
-            xb_t = keep.tile([P, 4, 1024], U8, name="xb%d" % T)
+            xb_t = keep.tile([P, 4, 1024], U8, name="xb%d" % T, align_bytes=256)
             xb.append(xb_t)
-        sc = keep.tile([P, 1024], F32, name="sc")
-        wr = keep.tile([P, 2, 4, 1024], BF16, name="wr")
-        wg = keep.tile([P, 4, 2, 1024], BF16, name="wg", align_bytes=ALB)
-        wc = keep.tile([P, 4, 2, 256], U32, name="wc", align_bytes=ALB)
-        ws = keep.tile([P, 4, 2, 256], U8, name="ws", align_bytes=ALB)
-        inf = keep.tile([P, 4, 8, 128], BF16, name="inf")
-        inflT = keep.tile([P, 4096], BF16, name="inflT")
-        dc = keep.tile([P, 4, 1024], BF16, name="dc")
-        brows = keep.tile([P, P], BF16, name="brows")
-        bias = keep.tile([P, 8], F32, name="bias")
-        brow = keep.tile([P, 1024], BF16, name="brow")
-        ident_f = keep.tile([P, P], F32, name="ident_f")
-        ident_b = keep.tile([P, P], BF16, name="ident_b")
-        warm = keep.tile([P, 2], F32, name="warm")
+        sc = keep.tile([P, 1024], F32, name="sc", align_bytes=256)
+        wr = keep.tile([P, 2, 4, 1024], BF16, name="wr", align_bytes=256)
+        wg = keep.tile([P, 4, 2, 1024], BF16, name="wg", align_bytes=256)
+        wc = keep.tile([P, 4, 2, 256], U32, name="wc", align_bytes=256)
+        ws = keep.tile([P, 4, 2, 256], U8, name="ws", align_bytes=256)
+        inf = keep.tile([P, 4, 8, 128], BF16, name="inf", align_bytes=256)
+        inflT = keep.tile([P, 4096], BF16, name="inflT", align_bytes=256)
+        dc = keep.tile([P, 4, 1024], BF16, name="dc", align_bytes=256)
+        brows = keep.tile([P, P], BF16, name="brows", align_bytes=256)
+        bias = keep.tile([P, 8], F32, name="bias", align_bytes=256)
+        brow = keep.tile([P, 1024], BF16, name="brow", align_bytes=256)
+        ident_f = keep.tile([P, P], F32, name="ident_f", align_bytes=256)
+        ident_b = keep.tile([P, P], BF16, name="ident_b", align_bytes=256)
+        warm = keep.tile([P, 2], F32, name="warm", align_bytes=256)
 
         nc.scalar.dma_start(out=sc[:], in_=x_scale.rearrange("a b k -> (a b k)").partition_broadcast(P))
         nc.gpsimd.memset(brows[:], 0.0)
@@ -213,18 +213,17 @@ def tile_splatinformationflow_pb_kernel(tc, x_bytes, x_scale, infl, dec, gate_w,
         def widen(m):
             T, j = m // 4, m % 4
             if j == 0:
-                xw_t = work.tile([P, 4, 1024], BF16, name="xw", tag="xw", bufs=2)
+                xw_t = work.tile([P, 4, 1024], BF16, name="xw", tag="xw", bufs=2, align_bytes=256)
                 xw[T] = xw_t
             nc.vector.tensor_tensor(out=xw[T][:, j, :], in0=xb[T][:, j, :].bitcast(FP8), in1=sc[:], op=ALU.mult)
 
         def x_order(m):
             T, j = m // 4, m % 4
-            if j == 0:
-                xp_t = work.tile([P, 4, 2, 2, 128], F32, name="xp", tag="xp", bufs=2)
-                xp[T] = xp_t
+            xp_t = work.tile([P, 2, 2, 128], F32, name="xp", tag="xp", bufs=4, align_bytes=256)
+            xp[m] = xp_t
             words = xw[T][:].rearrange("p j k -> p (j k)").bitcast(F32)
             nc.gpsimd.tensor_copy(
-                out=xp[T][:, j],
+                out=xp_t[:],
                 in_=words[:, 512 * j:512 * (j + 1)].rearrange("p (g i u) -> p g u i", g=2, u=2),
             )
 
@@ -236,13 +235,13 @@ def tile_splatinformationflow_pb_kernel(tc, x_bytes, x_scale, infl, dec, gate_w,
             for g in range(2):
                 for u in range(2):
                     lo = 512 * j + 256 * g
-                    src = xp[T][:, j, g, u, :] if m >= FIRST_ORDERED and m % 4 not in NOORD else words[:, lo + u:lo + 256:2]
+                    src = xp[m][:, g, u, :] if m >= FIRST_ORDERED and m % 4 not in NOORD else words[:, lo + u:lo + 256:2]
                     nc.tensor.transpose(xt_t[:, g, u, :], src, ident_f[:])
 
         def x_evac(eng, m):
             T, j = m // 4, m % 4
             if j == 0:
-                gr_t = work.tile([P, 2, 2048], BF16, name="gr", tag="gr", bufs=2, align_bytes=ALB)
+                gr_t = work.tile([P, 2, 2048], BF16, name="gr", tag="gr", bufs=2, align_bytes=256)
                 gr[T] = gr_t
             gw = gr[T][:].rearrange("p g c -> p (g c)").bitcast(F32).rearrange("p (g r u) -> p g r u", g=2, u=2)
             dst = gw[:, :, 128 * j:128 * (j + 1), :]
@@ -253,8 +252,8 @@ def tile_splatinformationflow_pb_kernel(tc, x_bytes, x_scale, infl, dec, gate_w,
                 nc.vector.tensor_copy(out=dst, in_=src)
 
         def x_quant(T):
-            xc_t = work.tile([P, 2, 512], U32, name="xc", tag="xc", bufs=3, align_bytes=ALB)
-            xs_t = work.tile([P, 2, 512], U8, name="xs", tag="xs", bufs=3, align_bytes=ALB)
+            xc_t = work.tile([P, 2, 512], U32, name="xc", tag="xc", bufs=3, align_bytes=256)
+            xs_t = work.tile([P, 2, 512], U8, name="xs", tag="xs", bufs=3, align_bytes=256)
             xc[T] = xc_t
             xs[T] = xs_t
             nc.vector.quantize_mx(
@@ -265,8 +264,8 @@ def tile_splatinformationflow_pb_kernel(tc, x_bytes, x_scale, infl, dec, gate_w,
 
         def x_quant_half(T, half):
             if half == 0:
-                xc_t = work.tile([P, 2, 512], U32, name="xc", tag="xc", bufs=3, align_bytes=ALB)
-                xs_t = work.tile([P, 2, 512], U8, name="xs", tag="xs", bufs=3, align_bytes=ALB)
+                xc_t = work.tile([P, 2, 512], U32, name="xc", tag="xc", bufs=3, align_bytes=256)
+                xs_t = work.tile([P, 2, 512], U8, name="xs", tag="xs", bufs=3, align_bytes=256)
                 xc[T] = xc_t
                 xs[T] = xs_t
             for g in range(2):
@@ -300,7 +299,7 @@ def tile_splatinformationflow_pb_kernel(tc, x_bytes, x_scale, infl, dec, gate_w,
                 )
 
         def sigmoid(c):
-            gt_t = work.tile([P, 512], F32, name="gt", tag="gt", bufs=4)
+            gt_t = work.tile([P, 512], F32, name="gt", tag="gt", bufs=4, align_bytes=256)
             gt[c] = gt_t
             nc.scalar.activation(out=gt_t[:], in_=acc[c][:], func=ACT.Sigmoid, bias=bias[:, c:c + 1], scale=1.0)
 
@@ -313,7 +312,7 @@ def tile_splatinformationflow_pb_kernel(tc, x_bytes, x_scale, infl, dec, gate_w,
             )
 
         def product(T, c):
-            ot_t = work.tile([P, 512], F32, name="ot_sb", tag="ot_sb", bufs=4)
+            ot_t = work.tile([P, 512], F32, name="ot_sb", tag="ot_sb", bufs=4, align_bytes=256)
             ot_sb[(T, c)] = ot_t
             nc.vector.tensor_tensor(out=ot_t[:], in0=fl[c][:], in1=gt[c][:], op=ALU.mult)
 
@@ -349,7 +348,7 @@ def tile_splatinformationflow_pb_kernel(tc, x_bytes, x_scale, infl, dec, gate_w,
 
         def row_add(c):
             i, h = c
-            zb_t = work.tile([P, 2, 256], F32, name="zb", tag="zb", bufs=2)
+            zb_t = work.tile([P, 2, 256], F32, name="zb", tag="zb", bufs=2, align_bytes=256)
             gt[c] = zb_t
             nc.vector.tensor_tensor(
                 out=zb_t[:], in0=acc[c][:],
@@ -357,7 +356,7 @@ def tile_splatinformationflow_pb_kernel(tc, x_bytes, x_scale, infl, dec, gate_w,
             )
 
         def row_sigmoid(c):
-            g_t = work.tile([P, 2, 256], F32, name="gt", tag="gt", bufs=4)
+            g_t = work.tile([P, 2, 256], F32, name="gt", tag="gt", bufs=4, align_bytes=256)
             nc.scalar.activation(out=g_t[:], in_=gt[c][:], func=ACT.Sigmoid)
             gt[c] = g_t
 
@@ -374,7 +373,7 @@ def tile_splatinformationflow_pb_kernel(tc, x_bytes, x_scale, infl, dec, gate_w,
 
         def o_tile(T):
             if T not in o_sb:
-                o_t = work.tile([P, 4, 1024], F32, name="o_sb", tag="o_sb", bufs=3)
+                o_t = work.tile([P, 4, 1024], F32, name="o_sb", tag="o_sb", bufs=3, align_bytes=256)
                 o_sb[T] = o_t
             return o_sb[T]
 

@@ -47,13 +47,18 @@ EVE = "S"
 WC = ('V', 'V', 'V', 'S')
 ST = 2
 TB = 1
-LASTV = 0
+LASTV = 1
 LASTS = ((0, 4), (1, 2), (3, 5), (6, 7))
 LASTR = (4, 5, 6, 7)
 RP = 3
 R0 = 1
+RA = 0
+RPB = 0
+RS = 0
+WV = (1, 2)
+WF = (1, 2, 3)
+WVP = 1
 WLOAD = 256
-ALB = 256
 LG = (99, 99)
 NOORD = (1, 3)
 GK = (0, 1, 0, 1, 0, 1, 5, 7)
@@ -416,6 +421,8 @@ def tile_splatinformationflow_pb_kernel(tc, x_bytes, x_scale, infl, dec, gate_w,
             x_evac("S", 3)
             infl_transpose(0)
             x_quant_half(0, 1)
+            if WAT[0] == 0 and WC[1] == "V" and 1 in WV:
+                w_copy("V", 1, 1)
             widen(4)
         else:
             widen(0)
@@ -443,17 +450,25 @@ def tile_splatinformationflow_pb_kernel(tc, x_bytes, x_scale, infl, dec, gate_w,
             x_evac(EV3, 3)
             infl_transpose(0)
             x_quant_half(0, 1)
+            if WAT[0] == 0 and WC[1] == "V" and 1 in WV:
+                w_copy("V", 1, 1)
             if not (EV3 == "V" and W4):
                 widen(4)
         n_wide, n_tr, n_ev, n_quant = 5, 4, 4, 1
 
         pend = []
+        copied = []
         for q in range(0, NQ + 1):
             T = q // 4
             slots = SLOT(q)
             prev = SLOT(q - 1)
             Tp = (q - 1) // 4
             late = []
+            for i in range(1, 4):
+                if q == WAT[i - 1] and i in WF:
+                    w_copy("S", i, 0)
+                    if WC[i] == "S":
+                        w_copy("S", i, 1)
             while n_ev < n_tr:
                 if q >= QV and q % 8 in VE:
                     x_evac("V", n_ev)
@@ -464,8 +479,10 @@ def tile_splatinformationflow_pb_kernel(tc, x_bytes, x_scale, infl, dec, gate_w,
                 n_ev += 1
             for i in range(1, 4):
                 if q == WAT[i - 1]:
-                    w_copy("S", i, 0)
-                    w_copy(WC[i], i, 1)
+                    if i not in WF:
+                        w_copy("S", i, 0)
+                    if not (WC[i] == "V" and i in WV) and not (WC[i] == "S" and i in WF):
+                        w_copy(WC[i], i, 1)
             now = [(T, c) for c, form in slots if form == "R"]
             todo = now if RSKEW == 0 else pend
             if TO == 0:
@@ -523,8 +540,8 @@ def tile_splatinformationflow_pb_kernel(tc, x_bytes, x_scale, infl, dec, gate_w,
                     if form == "F":
                         flow_mm(T, c)
                     (gate_mm if form == "F" else row_mm)(T, c)
-            for c, form in slots:
-                if form == "R":
+            if RA == 0:
+                for TT, c in now:
                     row_add(c)
             for c, form in slots:
                 if form == "F":
@@ -543,12 +560,26 @@ def tile_splatinformationflow_pb_kernel(tc, x_bytes, x_scale, infl, dec, gate_w,
                 x_quant(n_quant)
                 n_quant += 1
                 doq = False
-            for c, form in slots:
+            if RPB:
+                for TT, c in todo:
+                    row_product(TT, c)
+                    row_store(TT, c)
+            for s, (c, form) in enumerate(slots):
                 if form == "F":
                     product(T, c)
-            for TT, c in todo:
-                row_product(TT, c)
-                row_store(TT, c)
+                    if RA == 1 and s == 0:
+                        for TT, c2 in now:
+                            row_add(c2)
+            if RA == 2 or (RA == 1 and slots and slots[0][1] == "R"):
+                for TT, c in now:
+                    row_add(c)
+            if not RPB:
+                for TT, c in todo:
+                    row_product(TT, c)
+                    row_store(TT, c)
+            if RA == 3:
+                for TT, c in now:
+                    row_add(c)
             for c, form in prev:
                 if form == "F":
                     o_transpose(Tp, c, "xt" if q == NQ else "ot_ps")
@@ -562,6 +593,9 @@ def tile_splatinformationflow_pb_kernel(tc, x_bytes, x_scale, infl, dec, gate_w,
                     x_evac(EVE, n_ev)
                     n_ev += 1
                 doq = n_quant < NG and n_ev >= 4 * n_quant + 4
+            if RS == 1:
+                for TT, c in now:
+                    row_sigmoid(c)
             for s, (c, form) in enumerate(prev):
                 if form == "F":
                     o_evac("V" if (s == 1 and q >= 29 and LASTV) or (s == 1 and q % 8 in OV and q >= 8) else "S", Tp, c)
@@ -574,7 +608,7 @@ def tile_splatinformationflow_pb_kernel(tc, x_bytes, x_scale, infl, dec, gate_w,
                         store(Tp, fs[-1] - 3, fs[-1] + 1)
                 elif len(fs) == 2 or fs[0] % 2 == 1:
                     store(Tp, fs[-1] - 1, fs[-1] + 1)
-            if RSKEW:
+            if RS == 0:
                 for TT, c in now:
                     row_sigmoid(c)
             pend = now
@@ -585,12 +619,23 @@ def tile_splatinformationflow_pb_kernel(tc, x_bytes, x_scale, infl, dec, gate_w,
                 n_quant += 1
                 doq = False
             started = 0
+            for i in range(1, 4):
+                if q == WAT[i - 1] - 1 and WC[i] == "V" and i in WV and WVP == 0:
+                    w_copy("V", i, 1)
             while n_wide < min(NU, WLIM(q)) and started < ST:
                 widen(n_wide)
                 if n_wide >= FIRST_ORDERED and n_wide % 4 not in NOORD:
                     x_order(n_wide)
                 n_wide += 1
                 started += 1
+                if started == 1 and WVP == 1:
+                    for i in range(1, 4):
+                        if q == WAT[i - 1] - 1 and WC[i] == "V" and i in WV:
+                            w_copy("V", i, 1)
+                            copied.append(i)
+            for i in range(1, 4):
+                if WVP == 1 and q == WAT[i - 1] - 1 and WC[i] == "V" and i in WV and i not in copied:
+                    w_copy("V", i, 1)
             if doq and QA == 1:
                 x_quant(n_quant)
                 n_quant += 1

from contextlib import ExitStack

import concourse.mybir as mybir
from concourse.masks import make_identity

B, S, D, KS = 4, 1024, 1024, 128
def SLOT(q):
    if q < 0 or q >= 32:
        return ()
    T, pi = q // 4, q % 4
    return GS[GK[T]][pi]


def XLIM(q):
    return XA[q] if q < len(XA) else max(XA[-1], q + 6 - XB + (q >= LG[0]) + (q >= LG[1]))


def WLIM(q):
    return WA[q] if q < len(WA) else max(WA[-1], q + 6 - XB + WB + (q >= LG[0]) + (q >= LG[1]))


FLOPS = 2 * B * S * D * D + 2 * B * S * KS * D

F32 = mybir.dt.float32
BF16 = mybir.dt.bfloat16
U32 = mybir.dt.uint32
U8 = mybir.dt.uint8
FP8 = mybir.dt.float8_e4m3fn
FP8X4 = mybir.dt.float8_e4m3fn_x4
ACT = mybir.ActivationFunctionType
ALU = mybir.AluOpType

P = 128
NG = 8
NU = 32
VE = ()
XA = (6, 8, 9)
WA = (7, 9, 10)
XB = -1
WB = 2
ORD = 0
SEQ = [(0, 0), (0, 1), (0, 2), (0, 3), (1, 0), (1, 1), (1, 2), (1, 3)] if ORD == 0 else [(0, 0), (0, 1), (0, 2), (1, 0), (1, 1), (1, 2), (0, 3), (1, 3)] if ORD == 1 else [(0, 0), (0, 1), (1, 0), (1, 1), (0, 2), (1, 2), (0, 3), (1, 3)]
SEQ = SEQ + [(t, p) for t in range(2, 8) for p in range(4)]
WAT = (0, 1, 2)
EVN = ()
EVE = "S"
WC = ('V', 'V', 'V', 'S')
ST = 2
TB = 1
LASTV = 1
LASTS = ((0, 4), (1, 2), (3, 5), (6, 7))
LASTR = (4, 5, 6, 7)
RP = 3
R0 = 1
RA = 0
RPB = 0
RS = 0
WV = (1, 2)
WF = (1, 2, 3)
WVP = 1
WLOAD = 256
LG = (99, 99)
NOORD = (1, 3)
GK = (0, 1, 0, 1, 0, 1, 5, 7)
GS0 = (((0, "F"), (1, "F")), ((2, "F"), (3, "F")), ((4, "F"), (5, "F")), ((6, "F"), (7, "F")))
GS1 = (((0, "F"), (1, "F")), ((2, "F"), (3, "F")), ((4, "F"), ((3, 0), "R")), ((5, "F"), ((3, 1), "R")))
GS2 = (((0, "F"), ((2, 0), "R")), ((1, "F"), ((2, 1), "R")), ((2, "F"), ((3, 0), "R")), ((3, "F"), ((3, 1), "R")))
GS3 = (((0, "F"), ((1, 0), "R")), ((1, "F"), ((1, 1), "R")), (((2, 0), "R"), ((2, 1), "R")), (((3, 0), "R"), ((3, 1), "R")))
GS4 = (((0, "F"), ((3, 0), "R")), ((1, "F"), ((3, 1), "R")), ((2, "F"), (3, "F")), ((4, "F"), (5, "F")))
GS5 = (((0, "F"), ((2, 0), "R")), ((1, "F"), (2, "F")), ((3, "F"), ((2, 1), "R")), (((3, 0), "R"), ((3, 1), "R")))
GS6 = ((((3, 0), "R"), ((3, 1), "R")), (((2, 0), "R"), ((2, 1), "R")), ((0, "F"), (1, "F")), ((2, "F"), (3, "F")))
GS7 = (((0, "F"), ((2, 0), "R")), ((1, "F"), ((2, 1), "R")), ((2, "F"), (3, "F")), (((3, 0), "R"), ((3, 1), "R")))
GS8 = (((0, "F"), ((3, 0), "R")), ((1, "F"), (2, "F")), ((3, "F"), ((3, 1), "R")), ((4, "F"), (5, "F")))
GS9 = (((0, "F"), ((2, 0), "R")), ((1, "F"), ((2, 1), "R")), ((2, "F"), ((3, 0), "R")), (((3, 1), "R"), (3, "F")))
GS10 = ((((2, 0), "R"), ((2, 1), "R")), ((0, "F"), (1, "F")), ((2, "F"), ((3, 0), "R")), ((3, "F"), ((3, 1), "R")))
GS11 = (((0, "F"), ((2, 0), "R")), (((2, 1), "R"), (1, "F")), (((3, 0), "R"), ((3, 1), "R")), ((2, "F"), (3, "F")))
GS12 = (((0, "F"), (1, "F")), ((2, "F"), ((2, 0), "R")), ((3, "F"), ((2, 1), "R")), (((3, 0), "R"), ((3, 1), "R")))
GS13 = (((0, "F"), ((1, 0), "R")), ((1, "F"), ((1, 1), "R")), (((2, 0), "R"), ((2, 1), "R")), (((3, 0), "R"), ((3, 1), "R")))
GS14 = (((0, "F"), (1, "F")), ((2, "F"), ((3, 0), "R")), ((3, "F"), ((3, 1), "R")), ((4, "F"), (5, "F")))
GS = (GS0, GS1, GS2, GS3, GS4, GS5, GS6, GS7, GS8, GS9, GS10, GS11, GS12, GS13, GS14)
RC = (5,)
TO = 0
SH = 2
TG = {"xt": "xt", "acc": "acc", "fl": "fl", "ot_ps": "ot_ps"} if SH == 0 else {"xt": "ox", "acc": "acc", "fl": "fl", "ot_ps": "ox"} if SH == 1 else {"xt": "b", "acc": "b", "fl": "b", "ot_ps": "b"} if SH == 2 else {"xt": "ox", "acc": "af", "fl": "af", "ot_ps": "ox"} if SH == 3 else {"xt": "xt", "acc": "b", "fl": "b", "ot_ps": "b"}
BF = {"xt": 2, "acc": 2, "fl": 2, "ot_ps": 2} if SH == 0 else {"xt": 4, "acc": 2, "fl": 2, "ot_ps": 4} if SH == 1 else {"xt": 8, "acc": 8, "fl": 8, "ot_ps": 8} if SH == 2 else {"xt": 4, "acc": 4, "fl": 4, "ot_ps": 4} if SH == 3 else {"xt": 1, "acc": 7, "fl": 7, "ot_ps": 7}
RSKEW = 1
PENR = (4, 5, 6, 7)
PENS = ((0, 4), (1, 5), (2, 6), (3, 7))
RF = 0
RL = 7
IE = ("S", "S", "S", "S")
OV = ()
WBP = 0
HEAD = 1
EV3 = 'S'
W4 = 0
WPOS = (0, 2)
QV = 12
QL = 99
QE = 4
IT = (6, 14, 22)
QA = 0
FIRST_ORDERED = 12
NQ = 32


def tile_splatinformationflow_pb_kernel(tc, x_bytes, x_scale, infl, dec, gate_w, gate_b, out):
    nc = tc.nc

    x_view = x_bytes.rearrange("b (p h j) k -> b h p j k", h=2, j=4)
    out_view = out.rearrange("b (p h j) n -> b h p j n", h=2, j=4)
    infl_view = infl.rearrange("b (p q) k -> b p q k", q=8)
    w_view = gate_w.rearrange("(g p t) n -> g p t n", g=2, t=4)

    with ExitStack() as ctx:
        keep = ctx.enter_context(tc.tile_pool(name="keep", bufs=1))
        work = ctx.enter_context(tc.tile_pool(name="work", bufs=2))
        psum = ctx.enter_context(tc.psum_pool(name="psum", bufs=2))
        ctx.enter_context(tc.manual_schedule())

        xb = []
        for T in range(NG):
            xb_t = keep.tile([P, 4, 1024], U8, name="xb%d" % T, align_bytes=256)
            xb.append(xb_t)
        sc = keep.tile([P, 1024], F32, name="sc", align_bytes=256)
        wr = keep.tile([P, 2, 4, 1024], BF16, name="wr", align_bytes=256)
        wg = keep.tile([P, 4, 2, 1024], BF16, name="wg", align_bytes=256)
        wc = keep.tile([P, 4, 2, 256], U32, name="wc", align_bytes=256)
        ws = keep.tile([P, 4, 2, 256], U8, name="ws", align_bytes=256)
        inf = keep.tile([P, 4, 8, 128], BF16, name="inf", align_bytes=256)
        inflT = keep.tile([P, 4096], BF16, name="inflT", align_bytes=256)
        dc = keep.tile([P, 4, 1024], BF16, name="dc", align_bytes=256)
        brows = keep.tile([P, P], BF16, name="brows", align_bytes=256)
        bias = keep.tile([P, 8], F32, name="bias", align_bytes=256)
        brow = keep.tile([P, 1024], BF16, name="brow", align_bytes=256)
        ident_f = keep.tile([P, P], F32, name="ident_f", align_bytes=256)
        ident_b = keep.tile([P, P], BF16, name="ident_b", align_bytes=256)
        warm = keep.tile([P, 2], F32, name="warm", align_bytes=256)

        nc.scalar.dma_start(out=sc[:], in_=x_scale.rearrange("a b k -> (a b k)").partition_broadcast(P))
        nc.gpsimd.memset(brows[:], 0.0)
        nc.scalar.dma_start(out=brows[0:8, :], in_=gate_b.rearrange("(c n) -> c n", n=P))

        def load_x(T):
            nc.sync.dma_start(out=xb[T][:], in_=x_view[T // 2, T % 2])

        def load_x_unit(T, j):
            nc.sync.dma_start(out=xb[T][:, j, :], in_=x_view[T // 2, T % 2][:, j, :])

        def load_w(g, lo, hi):
            nc.sync.dma_start(out=wr[:, g, :, lo:hi], in_=w_view[g][:, :, lo:hi])

        def load_flow(b):
            nc.sync.dma_start(out=inf[:, b], in_=infl_view[b])
            nc.sync.dma_start(out=dc[:, b, :], in_=dec[b])

        if HEAD == 0:
            for j in range(4):
                load_x_unit(0, j)
            load_w(0, 0, 256)
            load_w(1, 0, 256)
        else:
            for j in range(4):
                load_x_unit(0, j)
                if j in WPOS:
                    load_w(WPOS.index(j), 0, WLOAD)
        load_flow(0)
        if WLOAD == 256:
            load_w(0, 256, 512)
            load_w(1, 256, 512)
        load_x(1)
        load_w(0, 512, 1024)
        load_w(1, 512, 1024)
        nc.sync.dma_start(out=brow[:], in_=gate_b.partition_broadcast(P))
        load_x(2)
        load_flow(1)
        load_x(3)
        load_x(4)
        load_flow(2)
        load_x(5)
        load_x(6)
        load_flow(3)
        load_x(7)

        make_identity(nc, ident_f[:])
        make_identity(nc, ident_b[:])
        nc.vector.memset(warm[:], 0.0)
        nc.scalar.activation(out=warm[:, 1:2], in_=warm[:, 0:1], func=ACT.Sigmoid)

        xw = {}
        xp = {}
        gr = {}
        xc = {}
        xs = {}
        xt = {}
        acc = {}
        fl = {}
        gt = {}
        ot_sb = {}
        ot_ps = {}
        o_sb = {}

        def w_copy(eng, i, g):
            dst = wg[:, i, g].rearrange("p (n t) -> p n t", t=4)
            src = wr[:, g, :, 256 * i:256 * (i + 1)].rearrange("p t n -> p n t")
            if eng == "S":
                nc.scalar.copy(out=dst, in_=src)
            else:
                nc.vector.tensor_copy(out=dst, in_=src)

        def w_quant(i):
            nc.vector.quantize_mx(
                out=wc[:, i].rearrange("p g n -> p (g n)").bitcast(FP8X4),
                scales=ws[:, i].rearrange("p g n -> p (g n)"),
                in_=wg[:, i].rearrange("p g c -> p (g c)"),
            )

        def widen(m):
            T, j = m // 4, m % 4
            if j == 0:
                xw_t = work.tile([P, 4, 1024], BF16, name="xw", tag="xw", bufs=2, align_bytes=256)
                xw[T] = xw_t
            nc.vector.tensor_tensor(out=xw[T][:, j, :], in0=xb[T][:, j, :].bitcast(FP8), in1=sc[:], op=ALU.mult)

        def x_order(m):
            T, j = m // 4, m % 4
            xp_t = work.tile([P, 2, 2, 128], F32, name="xp", tag="xp", bufs=4, align_bytes=256)
            xp[m] = xp_t
            words = xw[T][:].rearrange("p j k -> p (j k)").bitcast(F32)
            nc.gpsimd.tensor_copy(
                out=xp_t[:],
                in_=words[:, 512 * j:512 * (j + 1)].rearrange("p (g i u) -> p g u i", g=2, u=2),
            )

        def x_transpose(m):
            T, j = m // 4, m % 4
            xt_t = psum.tile([P, 2, 2, 128], F32, name="xt", tag=TG["xt"], bufs=BF["xt"])
            xt[m] = xt_t
            words = xw[T][:].rearrange("p j k -> p (j k)").bitcast(F32)
            for g in range(2):
                for u in range(2):
                    lo = 512 * j + 256 * g
                    src = xp[m][:, g, u, :] if m >= FIRST_ORDERED and m % 4 not in NOORD else words[:, lo + u:lo + 256:2]
                    nc.tensor.transpose(xt_t[:, g, u, :], src, ident_f[:])

        def x_evac(eng, m):
            T, j = m // 4, m % 4
            if j == 0:
                gr_t = work.tile([P, 2, 2048], BF16, name="gr", tag="gr", bufs=2, align_bytes=256)
                gr[T] = gr_t
            gw = gr[T][:].rearrange("p g c -> p (g c)").bitcast(F32).rearrange("p (g r u) -> p g r u", g=2, u=2)
            dst = gw[:, :, 128 * j:128 * (j + 1), :]
            src = xt[m][:].rearrange("p g u r -> p g r u")
            if eng == "S":
                nc.scalar.copy(out=dst, in_=src)
            else:
                nc.vector.tensor_copy(out=dst, in_=src)

        def x_quant(T):
            xc_t = work.tile([P, 2, 512], U32, name="xc", tag="xc", bufs=3, align_bytes=256)
            xs_t = work.tile([P, 2, 512], U8, name="xs", tag="xs", bufs=3, align_bytes=256)
            xc[T] = xc_t
            xs[T] = xs_t
            nc.vector.quantize_mx(
                out=xc_t[:].rearrange("p g n -> p (g n)").bitcast(FP8X4),
                scales=xs_t[:].rearrange("p g n -> p (g n)"),
                in_=gr[T][:].rearrange("p g c -> p (g c)"),
            )

        def x_quant_half(T, half):
            if half == 0:
                xc_t = work.tile([P, 2, 512], U32, name="xc", tag="xc", bufs=3, align_bytes=256)
                xs_t = work.tile([P, 2, 512], U8, name="xs", tag="xs", bufs=3, align_bytes=256)
                xc[T] = xc_t
                xs[T] = xs_t
            for g in range(2):
                nc.vector.quantize_mx(
                    out=xc[T][:, g, 256 * half:256 * (half + 1)].bitcast(FP8X4),
                    scales=xs[T][:, g, 256 * half:256 * (half + 1)],
                    in_=gr[T][:, g, 1024 * half:1024 * (half + 1)],
                )

        def infl_transpose(b):
            it = psum.tile([P, 8, 128], BF16, name="it", tag=TG["xt"], bufs=BF["xt"])
            for j in range(8):
                nc.tensor.transpose(it[:, j, :], inf[:, b, j, :], ident_b[:])
            if IE[b] == "S":
                nc.scalar.copy(out=inflT[:, 1024 * b:1024 * (b + 1)], in_=it[:].rearrange("p j r -> p (j r)"))
            else:
                nc.vector.tensor_copy(out=inflT[:, 1024 * b:1024 * (b + 1)], in_=it[:].rearrange("p j r -> p (j r)"))

        def gate_mm(T, c):
            acc_t = psum.tile([P, 512], F32, name="acc", tag=TG["acc"], bufs=BF["acc"])
            acc[c] = acc_t
            for g in range(2):
                nc.tensor.matmul_mx(
                    out=acc_t[:],
                    lhsT=wc[:, c // 2, g, 128 * (c % 2):128 * (c % 2 + 1)].bitcast(FP8X4),
                    lhsT_scale=ws[:, c // 2, g, 128 * (c % 2):128 * (c % 2 + 1)],
                    rhs=xc[T][:, g, :].bitcast(FP8X4),
                    rhs_scale=xs[T][:, g, :],
                    start=(g == 0),
                    stop=(g == 1),
                )

        def sigmoid(c):
            gt_t = work.tile([P, 512], F32, name="gt", tag="gt", bufs=4, align_bytes=256)
            gt[c] = gt_t
            nc.scalar.activation(out=gt_t[:], in_=acc[c][:], func=ACT.Sigmoid, bias=bias[:, c:c + 1], scale=1.0)

        def flow_mm(T, c):
            fl_t = psum.tile([P, 512], F32, name="fl", tag=TG["fl"], bufs=BF["fl"])
            fl[c] = fl_t
            nc.tensor.matmul(
                fl_t[:], lhsT=dc[:, T // 2, 128 * c:128 * (c + 1)], rhs=inflT[:, 512 * T:512 * (T + 1)],
                start=True, stop=True,
            )

        def product(T, c):
            ot_t = work.tile([P, 512], F32, name="ot_sb", tag="ot_sb", bufs=4, align_bytes=256)
            ot_sb[(T, c)] = ot_t
            nc.vector.tensor_tensor(out=ot_t[:], in0=fl[c][:], in1=gt[c][:], op=ALU.mult)

        def o_transpose(T, c, tag="ot_ps"):
            ps = psum.tile([P, 4, 128], F32, name="ot_ps", tag=TG[tag], bufs=BF[tag])
            ot_ps[(T, c)] = ps
            for j in range(4):
                nc.tensor.transpose(ps[:, j, :], ot_sb[(T, c)][:, 128 * j:128 * (j + 1)], ident_f[:])

        def o_evac(eng, T, c):
            o_tile(T)
            if eng == "S":
                nc.scalar.copy(out=o_sb[T][:, :, 128 * c:128 * (c + 1)], in_=ot_ps[(T, c)][:])
            else:
                nc.vector.tensor_copy(out=o_sb[T][:, :, 128 * c:128 * (c + 1)], in_=ot_ps[(T, c)][:])

        def row_mm(T, c):
            i, h = c
            z_t = psum.tile([P, 2, 256], F32, name="acc", tag=TG["acc"], bufs=BF["acc"])
            acc[c] = z_t
            for jj in range(2):
                for g in range(2):
                    lo = 128 * (2 * h + jj)
                    nc.tensor.matmul_mx(
                        out=z_t[:, jj, :],
                        lhsT=xc[T][:, g, lo:lo + 128].bitcast(FP8X4),
                        lhsT_scale=xs[T][:, g, lo:lo + 128],
                        rhs=wc[:, i, g, :].bitcast(FP8X4),
                        rhs_scale=ws[:, i, g, :],
                        start=(g == 0),
                        stop=(g == 1),
                    )

        def row_add(c):
            i, h = c
            zb_t = work.tile([P, 2, 256], F32, name="zb", tag="zb", bufs=2, align_bytes=256)
            gt[c] = zb_t
            nc.vector.tensor_tensor(
                out=zb_t[:], in0=acc[c][:],
                in1=brow[:, 256 * i:256 * (i + 1)].unsqueeze(1).to_broadcast([P, 2, 256]), op=ALU.add,
            )

        def row_sigmoid(c):
            g_t = work.tile([P, 2, 256], F32, name="gt", tag="gt", bufs=4, align_bytes=256)
            nc.scalar.activation(out=g_t[:], in_=gt[c][:], func=ACT.Sigmoid)
            gt[c] = g_t

        def row_flow(T, c):
            i, h = c
            fl_t = psum.tile([P, 2, 256], F32, name="fl", tag=TG["fl"], bufs=BF["fl"])
            fl[c] = fl_t
            for jj in range(2):
                lo = 512 * T + 128 * (2 * h + jj)
                nc.tensor.matmul(
                    fl_t[:, jj, :], lhsT=inflT[:, lo:lo + 128], rhs=dc[:, T // 2, 256 * i:256 * (i + 1)],
                    start=True, stop=True,
                )

        def o_tile(T):
            if T not in o_sb:
                o_t = work.tile([P, 4, 1024], F32, name="o_sb", tag="o_sb", bufs=3, align_bytes=256)
                o_sb[T] = o_t
            return o_sb[T]

        def row_product(T, c):
            i, h = c
            nc.vector.tensor_tensor(
                out=o_tile(T)[:, 2 * h:2 * h + 2, 256 * i:256 * (i + 1)], in0=fl[c][:], in1=gt[c][:], op=ALU.mult,
            )

        def row_store(T, c):
            i, h = c
            nc.sync.dma_start(
                out=out_view[T // 2, T % 2][:, 2 * h:2 * h + 2, 256 * i:256 * (i + 1)],
                in_=o_sb[T][:, 2 * h:2 * h + 2, 256 * i:256 * (i + 1)],
            )

        def store(T, c_lo, c_hi):
            nc.sync.dma_start(
                out=out_view[T // 2, T % 2][:, :, 128 * c_lo:128 * c_hi],
                in_=o_sb[T][:, :, 128 * c_lo:128 * c_hi],
            )

        bt = psum.tile([P, P], BF16, name="bt", tag=TG["acc"], bufs=BF["acc"])
        nc.tensor.transpose(bt[:], brows[:], ident_b[:])
        if HEAD == 0:
            for m in range(4):
                widen(m)
            x_transpose(0)
            x_transpose(1)
            x_evac("S", 0)
            w_copy("S", 0, 0)
            x_evac("S", 1)
            x_transpose(2)
            x_evac("S", 2)
            x_transpose(3)
            w_copy("V", 0, 1)
            x_quant_half(0, 0)
            w_quant(0)
            nc.vector.tensor_copy(out=bias[:], in_=bt[:, 0:8])
            x_evac("S", 3)
            infl_transpose(0)
            x_quant_half(0, 1)
            if WAT[0] == 0 and WC[1] == "V" and 1 in WV:
                w_copy("V", 1, 1)
            widen(4)
        else:
            widen(0)
            widen(1)
            widen(2)
            widen(3)
            w_copy("S", 0, 0)
            x_transpose(0)
            if HEAD == 1:
                w_copy("S", 0, 1)
                x_evac("S", 0)
            else:
                x_evac("S", 0)
                w_copy("S", 0, 1)
            x_transpose(1)
            x_evac("S", 1)
            x_transpose(2)
            x_evac("S", 2)
            x_transpose(3)
            w_quant(0)
            x_quant_half(0, 0)
            nc.vector.tensor_copy(out=bias[:], in_=bt[:, 0:8])
            if EV3 == "V":
                widen(4) if W4 else None
            x_evac(EV3, 3)
            infl_transpose(0)
            x_quant_half(0, 1)
            if WAT[0] == 0 and WC[1] == "V" and 1 in WV:
                w_copy("V", 1, 1)
            if not (EV3 == "V" and W4):
                widen(4)
        n_wide, n_tr, n_ev, n_quant = 5, 4, 4, 1

        pend = []
        copied = []
        for q in range(0, NQ + 1):
            T = q // 4
            slots = SLOT(q)
            prev = SLOT(q - 1)
            Tp = (q - 1) // 4
            late = []
            for i in range(1, 4):
                if q == WAT[i - 1] and i in WF:
                    w_copy("S", i, 0)
                    if WC[i] == "S":
                        w_copy("S", i, 1)
            while n_ev < n_tr:
                if q >= QV and q % 8 in VE:
                    x_evac("V", n_ev)
                elif q >= QL:
                    late.append(n_ev)
                else:
                    x_evac("S", n_ev)
                n_ev += 1
            for i in range(1, 4):
                if q == WAT[i - 1]:
                    if i not in WF:
                        w_copy("S", i, 0)
                    if not (WC[i] == "V" and i in WV) and not (WC[i] == "S" and i in WF):
                        w_copy(WC[i], i, 1)
            now = [(T, c) for c, form in slots if form == "R"]
            todo = now if RSKEW == 0 else pend
            if TO == 0:
                for c, form in slots:
                    (gate_mm if form == "F" else row_mm)(T, c)
                for c, form in slots:
                    if form == "F":
                        flow_mm(T, c)
                for TT, c in todo:
                    row_flow(TT, c)
            elif TO == 1:
                for c, form in slots:
                    (gate_mm if form == "F" else row_mm)(T, c)
                    if form == "F":
                        flow_mm(T, c)
                for TT, c in todo:
                    row_flow(TT, c)
            elif TO == 5:
                gate_first = [c for c, form in slots if form == "F"]
                for c in gate_first[:1]:
                    gate_mm(T, c)
                for c in gate_first:
                    flow_mm(T, c)
                for TT, c in todo:
                    row_flow(TT, c)
                for c, form in slots:
                    if form == "R":
                        row_mm(T, c)
                    elif c not in gate_first[:1]:
                        gate_mm(T, c)
            elif TO == 6:
                for c, form in slots:
                    if form == "F":
                        gate_mm(T, c)
                for c, form in slots:
                    if form == "F":
                        flow_mm(T, c)
                for TT, c in todo:
                    row_flow(TT, c)
                for c, form in slots:
                    if form == "R":
                        row_mm(T, c)
            elif TO == 3:
                for TT, c in todo:
                    row_flow(TT, c)
                for c, form in slots:
                    if form == "F":
                        flow_mm(T, c)
                for c, form in slots:
                    (gate_mm if form == "F" else row_mm)(T, c)
            else:
                for TT, c in todo:
                    row_flow(TT, c)
                for c, form in slots:
                    if form == "F":
                        flow_mm(T, c)
                    (gate_mm if form == "F" else row_mm)(T, c)
            if RA == 0:
                for TT, c in now:
                    row_add(c)
            for c, form in slots:
                if form == "F":
                    sigmoid(c)
            if RSKEW == 0:
                for c, form in slots:
                    if form == "R":
                        row_sigmoid(c)
            for e in late:
                x_evac("S", e)
            for i in range(1, 4):
                if q == WAT[i - 1]:
                    w_quant(i)
            doq = n_quant < NG and n_ev >= 4 * n_quant + 4
            if doq and q < QE:
                x_quant(n_quant)
                n_quant += 1
                doq = False
            if RPB:
                for TT, c in todo:
                    row_product(TT, c)
                    row_store(TT, c)
            for s, (c, form) in enumerate(slots):
                if form == "F":
                    product(T, c)
                    if RA == 1 and s == 0:
                        for TT, c2 in now:
                            row_add(c2)
            if RA == 2 or (RA == 1 and slots and slots[0][1] == "R"):
                for TT, c in now:
                    row_add(c)
            if not RPB:
                for TT, c in todo:
                    row_product(TT, c)
                    row_store(TT, c)
            if RA == 3:
                for TT, c in now:
                    row_add(c)
            for c, form in prev:
                if form == "F":
                    o_transpose(Tp, c, "xt" if q == NQ else "ot_ps")
            started = 0
            while n_tr < min(NU, XLIM(q), n_wide) and started < 2:
                x_transpose(n_tr)
                n_tr += 1
                started += 1
            if q in EVN:
                while n_ev < n_tr:
                    x_evac(EVE, n_ev)
                    n_ev += 1
                doq = n_quant < NG and n_ev >= 4 * n_quant + 4
            if RS == 1:
                for TT, c in now:
                    row_sigmoid(c)
            for s, (c, form) in enumerate(prev):
                if form == "F":
                    o_evac("V" if (s == 1 and q >= 29 and LASTV) or (s == 1 and q % 8 in OV and q >= 8) else "S", Tp, c)
                    if GK[Tp] > 1:
                        store(Tp, c, c + 1)
            if prev and GK[Tp] < 2:
                fs = [c for c, form in prev if form == "F"]
                if Tp < NG - 1 and GK[Tp] == 0:
                    if (q - 1) % 2 == 1:
                        store(Tp, fs[-1] - 3, fs[-1] + 1)
                elif len(fs) == 2 or fs[0] % 2 == 1:
                    store(Tp, fs[-1] - 1, fs[-1] + 1)
            if RS == 0:
                for TT, c in now:
                    row_sigmoid(c)
            pend = now
            if q in IT:
                infl_transpose(IT.index(q) + 1)
            if doq and QA == 0:
                x_quant(n_quant)
                n_quant += 1
                doq = False
            started = 0
            for i in range(1, 4):
                if q == WAT[i - 1] - 1 and WC[i] == "V" and i in WV and WVP == 0:
                    w_copy("V", i, 1)
            while n_wide < min(NU, WLIM(q)) and started < ST:
                widen(n_wide)
                if n_wide >= FIRST_ORDERED and n_wide % 4 not in NOORD:
                    x_order(n_wide)
                n_wide += 1
                started += 1
                if started == 1 and WVP == 1:
                    for i in range(1, 4):
                        if q == WAT[i - 1] - 1 and WC[i] == "V" and i in WV:
                            w_copy("V", i, 1)
                            copied.append(i)
            for i in range(1, 4):
                if WVP == 1 and q == WAT[i - 1] - 1 and WC[i] == "V" and i in WV and i not in copied:
                    w_copy("V", i, 1)
            if doq and QA == 1:
                x_quant(n_quant)
                n_quant += 1
